import numpy as np
import ml_dtypes


def mxq(x, axis, fmt="e4m3"):
    dtype, down = {"e4m3": (ml_dtypes.float8_e4m3fn, 7), "e5m2": (ml_dtypes.float8_e5m2, 14)}[fmt]
    v = np.moveaxis(np.asarray(x, np.float32).astype(ml_dtypes.bfloat16).astype(np.float64), axis, -1)
    blocks = v.reshape(v.shape[:-1] + (-1, 32))
    amax = np.abs(blocks).max(-1, keepdims=True)
    byte = np.maximum(np.where(amax > 0, np.frexp(amax)[1] - 1 + 127, 0) - down, 1)
    scale = np.exp2(byte - 127.0)
    codes = (blocks / scale).astype(np.float32).astype(dtype).astype(np.float64)
    return np.moveaxis((codes * scale).reshape(v.shape), -1, axis)


WIDE = False


def mx_kscale(k):
    if not WIDE:
        return np.ones(k)
    levels = np.array([10, -10, 5, -5, 0])
    a = np.random.permutation(np.resize(levels, k // 512 * 4)).reshape(k // 512, 4)
    idx = np.arange(k)
    return np.exp2(a[idx // 512, idx % 128 // 32])


BF16 = ml_dtypes.bfloat16


def bf(x):
    return np.asarray(x, np.float32).astype(BF16)


def f64(x):
    return np.asarray(x).astype(np.float64)


E2M1 = np.array([0.0, 0.5, 1.0, 1.5, 2.0, 3.0, 4.0, 6.0, -0.0, -0.5, -1.0, -1.5, -2.0, -3.0, -4.0, -6.0])


def pack_weight(w, fmt):
    k, n = w.shape
    w = f64(bf(w)).reshape(k // 32, 32, n)
    amax = np.abs(w).max(1)
    if fmt == "e4m3":
        byte = np.frexp(amax)[1] - 1 + 127 - 7
    else:
        mant, ex = np.frexp(amax / 6.0)
        byte = np.where(mant > 0.5, ex, ex - 1) + 127
    byte = np.clip(np.where(amax > 0, byte, 1), 1, 254)
    scaled = (w * np.exp2(127.0 - byte)[:, None, :]).reshape(k, n).astype(np.float32)
    by_word = np.ascontiguousarray(scaled.reshape(k // 512, 128, 4, n).transpose(0, 1, 3, 2))
    if fmt == "e4m3":
        words = by_word.astype(ml_dtypes.float8_e4m3fn).view(np.uint8)
    else:
        c = by_word.astype(ml_dtypes.float4_e2m1fn).view(np.uint8) & 0xF
        words = c[..., 0::2] | (c[..., 1::2] << 4)
    return np.ascontiguousarray(words), np.ascontiguousarray(byte.astype(np.uint8).reshape(k // 512, 16, n))


def unpack_weight(words, scales, fmt):
    g, p, n, _ = words.shape
    if fmt == "e4m3":
        vals = np.ascontiguousarray(words).view(ml_dtypes.float8_e4m3fn).astype(np.float64)
    else:
        nib = np.empty((g, p, n, 4), np.uint8)
        nib[..., 0::2] = words & 0xF
        nib[..., 1::2] = words >> 4
        vals = E2M1[nib]
    vals = vals * np.repeat(np.exp2(scales.astype(np.float64) - 127.0), 8, axis=1)[..., None]
    return vals.transpose(0, 1, 3, 2).reshape(g * 512, n)


N, E, C = 2048, 1024, 512
DENSITY = 0.01
FMT = "e4m3"


def setup_inputs():
    s, t = mx_kscale(N), mx_kscale(C)
    member = np.random.uniform(size=(N, E)) < DENSITY
    node_features = bf(np.random.standard_normal((N, C)) / s[:, None] * t[None, :])
    incidence = bf(member * s[:, None])
    words, scales = pack_weight(np.random.standard_normal((C, C)) * np.sqrt(E) / np.sqrt(DENSITY * N * C) / t[:, None], FMT)
    return {"node_features": node_features,
            "incidence": incidence,
            "W1_words": words,
            "W1_scales": scales,
            "b1": bf(np.random.standard_normal(C) * 0.1 * np.sqrt(E)),
            "edge_attention": bf(1.0 + np.random.standard_normal(E))}


def reference(node_features, incidence, W1_words, W1_scales, b1, edge_attention):
    agg = mxq(f64(incidence), 0, "e4m3").T @ mxq(f64(node_features), 0, "e4m3")
    lin = (mxq(agg, 1, "e4m3") @ unpack_weight(W1_words, W1_scales, FMT)) + f64(b1)
    a = f64(edge_attention)
    e = np.exp(a - a.max())
    attn = e / e.sum()
    return lin * attn[:, None]

@@ -1,0 +1,205 @@
+from contextlib import ExitStack
+
+import concourse.mybir as mybir
+from concourse.masks import make_identity
+
+BF16 = mybir.dt.bfloat16
+F32 = mybir.dt.float32
+I32 = mybir.dt.int32
+U32 = mybir.dt.uint32
+U8 = mybir.dt.uint8
+FP8X4 = mybir.dt.float8_e4m3fn_x4
+ALU = mybir.AluOpType
+ACT = mybir.ActivationFunctionType
+AXIS = mybir.AxisListType
+
+P = 128
+PACK = 4
+K_PASS = P * PACK
+BANK = 512
+
+NODES = 2048
+EDGES = 1024
+CHANNELS = 512
+PASSES = NODES // K_PASS
+HALVES = EDGES // BANK
+TILES = BANK // P
+RUN = 4
+
+FLOPS = 2 * NODES * EDGES * CHANNELS + 2 * EDGES * CHANNELS * CHANNELS
+
+
+def regroup(copy, grouped, rows):
+    copy(
+        out=grouped.rearrange("p (g i) j -> p g j i", i=RUN),
+        in_=rows.rearrange("p j (g i) -> p g j i", i=RUN),
+    )
+
+
+def tile_heterogeneoustemporalhypergraphnn_pa_kernel(
+    tc, node_features, incidence, W1_words, W1_scales, b1, edge_attention, out
+):
+    nc = tc.nc
+    with ExitStack() as ctx:
+        keep = ctx.enter_context(tc.tile_pool(name="keep", bufs=1))
+        psum = ctx.enter_context(tc.psum_pool(name="psum", bufs=8))
+
+        ident_bf16 = keep.tile([P, P], BF16)
+        make_identity(nc, ident_bf16[:])
+        ident_f32 = keep.tile([P, P], F32)
+        make_identity(nc, ident_f32[:])
+        ones = keep.tile([P, P], BF16)
+        nc.gpsimd.memset(ones[:], 1.0)
+
+        logit_rows = keep.tile([P, P], BF16)
+        nc.gpsimd.memset(logit_rows[:], 0.0)
+        nc.scalar.dma_start(
+            out=logit_rows[0 : EDGES // P, :], in_=edge_attention.rearrange("(s p) -> s p", p=P)
+        )
+        bias_row = keep.tile([P, CHANNELS], BF16)
+        nc.gpsimd.memset(bias_row[:], 0.0)
+        nc.scalar.dma_start(out=bias_row[0:1, :], in_=b1.rearrange("(o n) -> o n", o=1))
+
+        feat_rows = []
+        inc_rows = []
+        for c in range(PASSES):
+            nodes = slice(c * K_PASS, (c + 1) * K_PASS)
+            feat = keep.tile([P, PACK, CHANNELS], BF16, name="feat_rows%d" % c)
+            nc.sync.dma_start(
+                out=feat[:], in_=node_features[nodes, :].rearrange("(p j) w -> p j w", j=PACK)
+            )
+            feat_rows.append(feat)
+            inc = keep.tile([P, PACK, EDGES], BF16, name="inc_rows%d" % c)
+            nc.sync.dma_start(
+                out=inc[:], in_=incidence[nodes, :].rearrange("(p j) w -> p j w", j=PACK)
+            )
+            inc_rows.append(inc)
+
+        w1_codes = keep.tile([P, CHANNELS], U32, align_bytes=64)
+        nc.sync.dma_start(
+            out=w1_codes[:].bitcast(I32),
+            in_=W1_words[0].rearrange("p n t -> p (n t)").bitcast(I32),
+        )
+        w1_scales = keep.tile([P, CHANNELS], U8, align_bytes=64)
+        nc.vector.memset(w1_scales[:].bitcast(I32), 0)
+        for quadrant in range(4):
+            nc.sync.dma_start(
+                out=w1_scales[32 * quadrant : 32 * quadrant + 4, :].bitcast(I32),
+                in_=W1_scales[0, 4 * quadrant : 4 * quadrant + 4, :].bitcast(I32),
+            )
+
+        def seen_by_all(column):
+            spread = psum.tile([P, P], F32, name="spread", tag="bank")
+            nc.tensor.matmul(
+                spread[:], lhsT=column.to_broadcast([P, P]), rhs=ident_f32[:], start=True, stop=True
+            )
+            return spread
+
+        n_tiles = EDGES // P
+        logit_cols_ps = psum.tile([P, P], BF16, tag="bank")
+        nc.tensor.transpose(logit_cols_ps[:], logit_rows[:], ident_bf16[:])
+        logit_cols = keep.tile([P, n_tiles], F32)
+        nc.vector.tensor_copy(out=logit_cols[:], in_=logit_cols_ps[:, 0:n_tiles])
+        part_max = keep.tile([P, 1], F32)
+        nc.vector.reduce_max(out=part_max[:], in_=logit_cols[:], axis=AXIS.X)
+        neg_max = keep.tile([P, 1], F32)
+        nc.vector.reduce_max(out=neg_max[:], in_=seen_by_all(part_max[:])[:], axis=AXIS.X)
+        nc.vector.tensor_scalar_mul(out=neg_max[:], in0=neg_max[:], scalar1=-1.0)
+        exp_cols = keep.tile([P, n_tiles], F32)
+        part_sum = keep.tile([P, 1], F32)
+        nc.scalar.activation(
+            out=exp_cols[:], in_=logit_cols[:], func=ACT.Exp, bias=neg_max[:], scale=1.0,
+            accum_out=part_sum[:],
+        )
+        inv_sum = keep.tile([P, 1], F32)
+        nc.vector.reduce_sum(out=inv_sum[:], in_=seen_by_all(part_sum[:])[:], axis=AXIS.X)
+        nc.vector.reciprocal(out=inv_sum[:], in_=inv_sum[:])
+        attn = keep.tile([P, n_tiles], F32)
+        nc.vector.tensor_scalar_mul(out=attn[:], in0=exp_cols[:], scalar1=inv_sum[:])
+
+        bias_ps = psum.tile([P, CHANNELS], F32, tag="bank")
+        nc.tensor.matmul(bias_ps[:], lhsT=ones[:], rhs=bias_row[:], start=True, stop=True)
+        bias_all = keep.tile([P, CHANNELS], F32)
+        nc.scalar.copy(out=bias_all[:], in_=bias_ps[:])
+        bias_attn = []
+        for s in range(n_tiles):
+            scaled = keep.tile([P, CHANNELS], F32, name="bias_attn%d" % s)
+            nc.vector.tensor_scalar_mul(out=scaled[:], in0=bias_all[:], scalar1=attn[:, s : s + 1])
+            bias_attn.append(scaled)
+
+        acc = [
+            [psum.tile([P, BANK], F32, name="acc%d%d" % (h, t), tag="bank") for t in range(PACK)]
+            for h in range(HALVES)
+        ]
+        for c in range(PASSES):
+            feat_grouped = keep.tile([P, PACK, P, PACK], BF16, name="feat_grouped%d" % c, align_bytes=64)
+            nc.vector.tensor_copy(
+                out=feat_grouped[:].rearrange("p t q j -> p q j t"),
+                in_=feat_rows[c][:].rearrange("p j (q t) -> p q j t", t=PACK),
+            )
+            inc_grouped = keep.tile([P, EDGES, PACK], BF16, name="inc_grouped%d" % c, align_bytes=64)
+            for copy, cols in (
+                (nc.scalar.copy, slice(0, 512)),
+                (nc.scalar.copy, slice(512, 768)),
+                (nc.vector.tensor_copy, slice(768, 1024)),
+            ):
+                regroup(copy, inc_grouped[:, cols, :], inc_rows[c][:, :, cols])
+
+            feat_codes = keep.tile([P, CHANNELS], U32, name="feat_codes%d" % c, align_bytes=64)
+            feat_scales = keep.tile([P, CHANNELS], U8, name="feat_scales%d" % c, align_bytes=64)
+            nc.vector.quantize_mx(
+                out=feat_codes[:].bitcast(FP8X4),
+                scales=feat_scales[:],
+                in_=feat_grouped[:].rearrange("p t q j -> p (t q j)"),
+            )
+            inc_codes = keep.tile([P, EDGES], U32, name="inc_codes%d" % c, align_bytes=64)
+            inc_scales = keep.tile([P, EDGES], U8, name="inc_scales%d" % c, align_bytes=64)
+            for h in range(HALVES):
+                edges = slice(h * BANK, (h + 1) * BANK)
+                nc.vector.quantize_mx(
+                    out=inc_codes[:, edges].bitcast(FP8X4),
+                    scales=inc_scales[:, edges],
+                    in_=inc_grouped[:, edges, :].rearrange("p e j -> p (e j)"),
+                )
+                for t in range(PACK):
+                    nc.tensor.matmul_mx(
+                        out=acc[h][t][:],
+                        lhsT=feat_codes[:, t * P : (t + 1) * P].bitcast(FP8X4),
+                        lhsT_scale=feat_scales[:, t * P : (t + 1) * P],
+                        rhs=inc_codes[:, edges].bitcast(FP8X4),
+                        rhs_scale=inc_scales[:, edges],
+                        start=(c == 0),
+                        stop=(c == PASSES - 1),
+                    )
+
+        for h in range(HALVES):
+            agg_rows = keep.tile([P, PACK, BANK], BF16, name="agg_rows%d" % h)
+            for t in range(PACK):
+                nc.scalar.copy(out=agg_rows[:, t, :], in_=acc[h][t][:])
+            agg_grouped = keep.tile([P, BANK, PACK], BF16, name="agg_grouped%d" % h, align_bytes=64)
+            regroup(nc.vector.tensor_copy, agg_grouped[:], agg_rows[:])
+            agg_codes = keep.tile([P, BANK], U32, name="agg_codes%d" % h, align_bytes=64)
+            agg_scales = keep.tile([P, BANK], U8, name="agg_scales%d" % h, align_bytes=64)
+            nc.vector.quantize_mx(
+                out=agg_codes[:].bitcast(FP8X4),
+                scales=agg_scales[:],
+                in_=agg_grouped[:].rearrange("p e t -> p (e t)"),
+            )
+            for i in range(TILES):
+                s = h * TILES + i
+                lin = psum.tile([P, CHANNELS], F32, name="lin", tag="bank")
+                nc.tensor.matmul_mx(
+                    out=lin[:],
+                    lhsT=agg_codes[:, i * P : (i + 1) * P].bitcast(FP8X4),
+                    lhsT_scale=agg_scales[:, i * P : (i + 1) * P],
+                    rhs=w1_codes[:].bitcast(FP8X4),
+                    rhs_scale=w1_scales[:],
+                    start=True,
+                    stop=True,
+                )
+                result = keep.tile([P, CHANNELS], F32, name="result%d" % s)
+                nc.vector.scalar_tensor_tensor(
+                    out=result[:], in0=lin[:], scalar=attn[:, s : s + 1], in1=bias_attn[s][:],
+                    op0=ALU.mult, op1=ALU.add,
+                )
+                nc.sync.dma_start(out=out[s * P : (s + 1) * P, :], in_=result[:])

@@ -24,6 +24,8 @@ CHANNELS = 512
 PASSES = NODES // K_PASS
 HALVES = EDGES // BANK
 TILES = BANK // P
+INC_SCALAR_COLS = 384
+FEAT_SCALAR_Q = 64
 RUN = 4
 
 FLOPS = 2 * NODES * EDGES * CHANNELS + 2 * EDGES * CHANNELS * CHANNELS
@@ -49,31 +51,30 @@ def tile_heterogeneoustemporalhypergraphnn_pa_kernel(
         ident_f32 = keep.tile([P, P], F32)
         make_identity(nc, ident_f32[:])
         ones = keep.tile([P, P], BF16)
-        nc.gpsimd.memset(ones[:], 1.0)
+        nc.vector.memset(ones[:], 1.0)
 
         logit_rows = keep.tile([P, P], BF16)
-        nc.gpsimd.memset(logit_rows[:], 0.0)
-        nc.scalar.dma_start(
+        nc.vector.memset(logit_rows[:], 0.0)
+        nc.sync.dma_start(
             out=logit_rows[0 : EDGES // P, :], in_=edge_attention.rearrange("(s p) -> s p", p=P)
         )
         bias_row = keep.tile([P, CHANNELS], BF16)
-        nc.gpsimd.memset(bias_row[:], 0.0)
-        nc.scalar.dma_start(out=bias_row[0:1, :], in_=b1.rearrange("(o n) -> o n", o=1))
+        nc.vector.memset(bias_row[:], 0.0)
+        nc.sync.dma_start(out=bias_row[0:1, :], in_=b1.rearrange("(o n) -> o n", o=1))
 
-        feat_rows = []
-        inc_rows = []
-        for c in range(PASSES):
-            nodes = slice(c * K_PASS, (c + 1) * K_PASS)
-            feat = keep.tile([P, PACK, CHANNELS], BF16, name="feat_rows%d" % c)
-            nc.sync.dma_start(
-                out=feat[:], in_=node_features[nodes, :].rearrange("(p j) w -> p j w", j=PACK)
-            )
-            feat_rows.append(feat)
-            inc = keep.tile([P, PACK, EDGES], BF16, name="inc_rows%d" % c)
-            nc.sync.dma_start(
-                out=inc[:], in_=incidence[nodes, :].rearrange("(p j) w -> p j w", j=PACK)
-            )
-            inc_rows.append(inc)
+        def load_passes(source, width, name):
+            passes = []
+            for c in range(PASSES):
+                rows = keep.tile([P, PACK, width], BF16, name="%s%d" % (name, c))
+                nc.sync.dma_start(
+                    out=rows[:],
+                    in_=source[c * K_PASS : (c + 1) * K_PASS, :].rearrange("(p j) w -> p j w", j=PACK),
+                )
+                passes.append(rows)
+            return passes
+
+        feat_rows = load_passes(node_features, CHANNELS, "feat_rows")
+        inc_rows = load_passes(incidence, EDGES, "inc_rows")
 
         w1_codes = keep.tile([P, CHANNELS], U32, align_bytes=64)
         nc.sync.dma_start(
@@ -127,79 +128,82 @@ def tile_heterogeneoustemporalhypergraphnn_pa_kernel(
             nc.vector.tensor_scalar_mul(out=scaled[:], in0=bias_all[:], scalar1=attn[:, s : s + 1])
             bias_attn.append(scaled)
 
-        acc = [
-            [psum.tile([P, BANK], F32, name="acc%d%d" % (h, t), tag="bank") for t in range(PACK)]
-            for h in range(HALVES)
-        ]
+        feat_codes = []
+        feat_scales = []
         for c in range(PASSES):
-            feat_grouped = keep.tile([P, PACK, P, PACK], BF16, name="feat_grouped%d" % c, align_bytes=64)
-            nc.vector.tensor_copy(
-                out=feat_grouped[:].rearrange("p t q j -> p q j t"),
-                in_=feat_rows[c][:].rearrange("p j (q t) -> p q j t", t=PACK),
-            )
-            inc_grouped = keep.tile([P, EDGES, PACK], BF16, name="inc_grouped%d" % c, align_bytes=64)
-            for copy, cols in (
-                (nc.scalar.copy, slice(0, 512)),
-                (nc.scalar.copy, slice(512, 768)),
-                (nc.vector.tensor_copy, slice(768, 1024)),
-            ):
-                regroup(copy, inc_grouped[:, cols, :], inc_rows[c][:, :, cols])
-
-            feat_codes = keep.tile([P, CHANNELS], U32, name="feat_codes%d" % c, align_bytes=64)
-            feat_scales = keep.tile([P, CHANNELS], U8, name="feat_scales%d" % c, align_bytes=64)
-            nc.vector.quantize_mx(
-                out=feat_codes[:].bitcast(FP8X4),
-                scales=feat_scales[:],
-                in_=feat_grouped[:].rearrange("p t q j -> p (t q j)"),
-            )
-            inc_codes = keep.tile([P, EDGES], U32, name="inc_codes%d" % c, align_bytes=64)
-            inc_scales = keep.tile([P, EDGES], U8, name="inc_scales%d" % c, align_bytes=64)
-            for h in range(HALVES):
-                edges = slice(h * BANK, (h + 1) * BANK)
-                nc.vector.quantize_mx(
-                    out=inc_codes[:, edges].bitcast(FP8X4),
-                    scales=inc_scales[:, edges],
-                    in_=inc_grouped[:, edges, :].rearrange("p e j -> p (e j)"),
+            grouped = keep.tile([P, PACK, P, PACK], BF16, name="feat_grouped%d" % c, align_bytes=64)
+            for copy, first, last in ((nc.scalar.copy, 0, FEAT_SCALAR_Q), (nc.vector.tensor_copy, FEAT_SCALAR_Q, P)):
+                copy(
+                    out=grouped[:, :, first:last, :].rearrange("p t q j -> p q j t"),
+                    in_=feat_rows[c][:, :, PACK * first : PACK * last].rearrange("p j (q t) -> p q j t", t=PACK),
                 )
-                for t in range(PACK):
-                    nc.tensor.matmul_mx(
-                        out=acc[h][t][:],
-                        lhsT=feat_codes[:, t * P : (t + 1) * P].bitcast(FP8X4),
-                        lhsT_scale=feat_scales[:, t * P : (t + 1) * P],
-                        rhs=inc_codes[:, edges].bitcast(FP8X4),
-                        rhs_scale=inc_scales[:, edges],
-                        start=(c == 0),
-                        stop=(c == PASSES - 1),
-                    )
+            codes = keep.tile([P, CHANNELS], U32, name="feat_codes%d" % c, align_bytes=64)
+            scales = keep.tile([P, CHANNELS], U8, name="feat_scales%d" % c, align_bytes=64)
+            nc.vector.quantize_mx(
+                out=codes[:].bitcast(FP8X4),
+                scales=scales[:],
+                in_=grouped[:].rearrange("p t q j -> p (t q j)"),
+            )
+            feat_codes.append(codes)
+            feat_scales.append(scales)
 
-        for h in range(HALVES):
-            agg_rows = keep.tile([P, PACK, BANK], BF16, name="agg_rows%d" % h)
-            for t in range(PACK):
-                nc.scalar.copy(out=agg_rows[:, t, :], in_=acc[h][t][:])
-            agg_grouped = keep.tile([P, BANK, PACK], BF16, name="agg_grouped%d" % h, align_bytes=64)
-            regroup(nc.vector.tensor_copy, agg_grouped[:], agg_rows[:])
-            agg_codes = keep.tile([P, BANK], U32, name="agg_codes%d" % h, align_bytes=64)
-            agg_scales = keep.tile([P, BANK], U8, name="agg_scales%d" % h, align_bytes=64)
+        agg_ps = [psum.tile([P, PACK, P], F32, name="agg_ps%d" % s, tag="bank") for s in range(n_tiles)]
+        for c in range(PASSES):
+            for h in range(HALVES):
+                first = h * BANK
+                grouped = keep.tile([P, BANK, PACK], BF16, name="inc_grouped%d%d" % (c, h), align_bytes=64)
+                regroup(
+                    nc.scalar.copy,
+                    grouped[:, 0:INC_SCALAR_COLS, :],
+                    inc_rows[c][:, :, first : first + INC_SCALAR_COLS],
+                )
+                regroup(
+                    nc.vector.tensor_copy,
+                    grouped[:, INC_SCALAR_COLS:BANK, :],
+                    inc_rows[c][:, :, first + INC_SCALAR_COLS : first + BANK],
+                )
+                codes = keep.tile([P, BANK], U32, name="inc_codes%d%d" % (c, h), align_bytes=64)
+                scales = keep.tile([P, BANK], U8, name="inc_scales%d%d" % (c, h), align_bytes=64)
+                nc.vector.quantize_mx(
+                    out=codes[:].bitcast(FP8X4),
+                    scales=scales[:],
+                    in_=grouped[:].rearrange("p e j -> p (e j)"),
+                )
+                for i in range(TILES):
+                    for t in range(PACK):
+                        nc.tensor.matmul_mx(
+                            out=agg_ps[h * TILES + i][:, t, :],
+                            lhsT=feat_codes[c][:, t * P : (t + 1) * P].bitcast(FP8X4),
+                            lhsT_scale=feat_scales[c][:, t * P : (t + 1) * P],
+                            rhs=codes[:, i * P : (i + 1) * P].bitcast(FP8X4),
+                            rhs_scale=scales[:, i * P : (i + 1) * P],
+                            start=(c == 0 and t == 0),
+                            stop=(c == PASSES - 1 and t == PACK - 1),
+                        )
+
+        for s in range(n_tiles):
+            agg_grouped = keep.tile([P, P, PACK], BF16, name="agg_grouped%d" % s, align_bytes=64)
+            nc.scalar.copy(out=agg_grouped[:], in_=agg_ps[s][:].rearrange("p t e -> p e t"))
+            agg_codes = keep.tile([P, P], U32, name="agg_codes%d" % s, align_bytes=64)
+            agg_scales = keep.tile([P, P], U8, name="agg_scales%d" % s, align_bytes=64)
             nc.vector.quantize_mx(
                 out=agg_codes[:].bitcast(FP8X4),
                 scales=agg_scales[:],
                 in_=agg_grouped[:].rearrange("p e t -> p (e t)"),
             )
-            for i in range(TILES):
-                s = h * TILES + i
-                lin = psum.tile([P, CHANNELS], F32, name="lin", tag="bank")
-                nc.tensor.matmul_mx(
-                    out=lin[:],
-                    lhsT=agg_codes[:, i * P : (i + 1) * P].bitcast(FP8X4),
-                    lhsT_scale=agg_scales[:, i * P : (i + 1) * P],
-                    rhs=w1_codes[:].bitcast(FP8X4),
-                    rhs_scale=w1_scales[:],
-                    start=True,
-                    stop=True,
-                )
-                result = keep.tile([P, CHANNELS], F32, name="result%d" % s)
-                nc.vector.scalar_tensor_tensor(
-                    out=result[:], in0=lin[:], scalar=attn[:, s : s + 1], in1=bias_attn[s][:],
-                    op0=ALU.mult, op1=ALU.add,
-                )
-                nc.sync.dma_start(out=out[s * P : (s + 1) * P, :], in_=result[:])
+            lin = psum.tile([P, CHANNELS], F32, name="lin", tag="bank")
+            nc.tensor.matmul_mx(
+                out=lin[:],
+                lhsT=agg_codes[:].bitcast(FP8X4),
+                lhsT_scale=agg_scales[:],
+                rhs=w1_codes[:].bitcast(FP8X4),
+                rhs_scale=w1_scales[:],
+                start=True,
+                stop=True,
+            )
+            result = keep.tile([P, CHANNELS], F32, name="result%d" % s)
+            nc.vector.scalar_tensor_tensor(
+                out=result[:], in0=lin[:], scalar=attn[:, s : s + 1], in1=bias_attn[s][:],
+                op0=ALU.mult, op1=ALU.add,
+            )
+            nc.sync.dma_start(out=out[s * P : (s + 1) * P, :], in_=result[:])

@@ -23,19 +23,13 @@ EDGES = 1024
 CHANNELS = 512
 PASSES = NODES // K_PASS
 HALVES = EDGES // BANK
-TILES = BANK // P
-INC_SCALAR_COLS = 384
-FEAT_SCALAR_Q = 64
+TILES = EDGES // P
 RUN = 4
 
+INC_SCALAR_COLS = 320
+FEAT_SCALAR_Q = 64
+
 FLOPS = 2 * NODES * EDGES * CHANNELS + 2 * EDGES * CHANNELS * CHANNELS
-
-
-def regroup(copy, grouped, rows):
-    copy(
-        out=grouped.rearrange("p (g i) j -> p g j i", i=RUN),
-        in_=rows.rearrange("p j (g i) -> p g j i", i=RUN),
-    )
 
 
 def tile_heterogeneoustemporalhypergraphnn_pa_kernel(
@@ -45,36 +39,32 @@ def tile_heterogeneoustemporalhypergraphnn_pa_kernel(
     with ExitStack() as ctx:
         keep = ctx.enter_context(tc.tile_pool(name="keep", bufs=1))
         psum = ctx.enter_context(tc.psum_pool(name="psum", bufs=8))
+        ctx.enter_context(tc.manual_schedule())
 
-        ident_bf16 = keep.tile([P, P], BF16)
-        make_identity(nc, ident_bf16[:])
-        ident_f32 = keep.tile([P, P], F32)
-        make_identity(nc, ident_f32[:])
-        ones = keep.tile([P, P], BF16)
-        nc.vector.memset(ones[:], 1.0)
+        def load_pass(source, c, width, name):
+            rows = keep.tile([P, PACK, width], BF16, name="%s%d" % (name, c))
+            nc.sync.dma_start(
+                out=rows[:],
+                in_=source[c * K_PASS : (c + 1) * K_PASS, :].rearrange("(p j) w -> p j w", j=PACK),
+            )
+            return rows
+
+        feat_rows = [load_pass(node_features, 0, CHANNELS, "feat_rows")]
 
         logit_rows = keep.tile([P, P], BF16)
         nc.vector.memset(logit_rows[:], 0.0)
         nc.sync.dma_start(
-            out=logit_rows[0 : EDGES // P, :], in_=edge_attention.rearrange("(s p) -> s p", p=P)
+            out=logit_rows[0:TILES, :], in_=edge_attention.rearrange("(s p) -> s p", p=P)
         )
         bias_row = keep.tile([P, CHANNELS], BF16)
         nc.vector.memset(bias_row[:], 0.0)
         nc.sync.dma_start(out=bias_row[0:1, :], in_=b1.rearrange("(o n) -> o n", o=1))
 
-        def load_passes(source, width, name):
-            passes = []
-            for c in range(PASSES):
-                rows = keep.tile([P, PACK, width], BF16, name="%s%d" % (name, c))
-                nc.sync.dma_start(
-                    out=rows[:],
-                    in_=source[c * K_PASS : (c + 1) * K_PASS, :].rearrange("(p j) w -> p j w", j=PACK),
-                )
-                passes.append(rows)
-            return passes
-
-        feat_rows = load_passes(node_features, CHANNELS, "feat_rows")
-        inc_rows = load_passes(incidence, EDGES, "inc_rows")
+        inc_rows = []
+        for c in range(PASSES):
+            if c + 1 < PASSES:
+                feat_rows.append(load_pass(node_features, c + 1, CHANNELS, "feat_rows"))
+            inc_rows.append(load_pass(incidence, c, EDGES, "inc_rows"))
 
         w1_codes = keep.tile([P, CHANNELS], U32, align_bytes=64)
         nc.sync.dma_start(
@@ -89,6 +79,16 @@ def tile_heterogeneoustemporalhypergraphnn_pa_kernel(
                 in_=W1_scales[0, 4 * quadrant : 4 * quadrant + 4, :].bitcast(I32),
             )
 
+        ident_bf16 = keep.tile([P, P], BF16)
+        make_identity(nc, ident_bf16[:])
+        ident_f32 = keep.tile([P, P], F32)
+        make_identity(nc, ident_f32[:])
+        ones = keep.tile([P, P], BF16)
+        nc.vector.memset(ones[:], 1.0)
+        warm = keep.tile([P, 1], F32)
+        nc.vector.memset(warm[:], 0.0)
+        nc.scalar.activation(out=warm[:], in_=warm[:], func=ACT.Exp)
+
         def seen_by_all(column):
             spread = psum.tile([P, P], F32, name="spread", tag="bank")
             nc.tensor.matmul(
@@ -96,92 +96,132 @@ def tile_heterogeneoustemporalhypergraphnn_pa_kernel(
             )
             return spread
 
-        n_tiles = EDGES // P
-        logit_cols_ps = psum.tile([P, P], BF16, tag="bank")
-        nc.tensor.transpose(logit_cols_ps[:], logit_rows[:], ident_bf16[:])
-        logit_cols = keep.tile([P, n_tiles], F32)
-        nc.vector.tensor_copy(out=logit_cols[:], in_=logit_cols_ps[:, 0:n_tiles])
-        part_max = keep.tile([P, 1], F32)
-        nc.vector.reduce_max(out=part_max[:], in_=logit_cols[:], axis=AXIS.X)
-        neg_max = keep.tile([P, 1], F32)
-        nc.vector.reduce_max(out=neg_max[:], in_=seen_by_all(part_max[:])[:], axis=AXIS.X)
-        nc.vector.tensor_scalar_mul(out=neg_max[:], in0=neg_max[:], scalar1=-1.0)
-        exp_cols = keep.tile([P, n_tiles], F32)
-        part_sum = keep.tile([P, 1], F32)
-        nc.scalar.activation(
-            out=exp_cols[:], in_=logit_cols[:], func=ACT.Exp, bias=neg_max[:], scale=1.0,
-            accum_out=part_sum[:],
-        )
-        inv_sum = keep.tile([P, 1], F32)
-        nc.vector.reduce_sum(out=inv_sum[:], in_=seen_by_all(part_sum[:])[:], axis=AXIS.X)
-        nc.vector.reciprocal(out=inv_sum[:], in_=inv_sum[:])
-        attn = keep.tile([P, n_tiles], F32)
-        nc.vector.tensor_scalar_mul(out=attn[:], in0=exp_cols[:], scalar1=inv_sum[:])
-
-        bias_ps = psum.tile([P, CHANNELS], F32, tag="bank")
-        nc.tensor.matmul(bias_ps[:], lhsT=ones[:], rhs=bias_row[:], start=True, stop=True)
+        logit_cols = keep.tile([P, TILES], F32)
+        exp_cols = keep.tile([P, TILES], F32)
+        attn = keep.tile([P, TILES], F32)
         bias_all = keep.tile([P, CHANNELS], F32)
-        nc.scalar.copy(out=bias_all[:], in_=bias_ps[:])
+
+        def softmax_partition_max():
+            logit_cols_ps = psum.tile([P, P], BF16, tag="bank")
+            nc.tensor.transpose(logit_cols_ps[:], logit_rows[:], ident_bf16[:])
+            nc.vector.tensor_copy(out=logit_cols[:], in_=logit_cols_ps[:, 0:TILES])
+            part_max = keep.tile([P, 1], F32)
+            nc.vector.reduce_max(out=part_max[:], in_=logit_cols[:], axis=AXIS.X)
+            bias_ps = psum.tile([P, CHANNELS], F32, tag="bank")
+            nc.tensor.matmul(bias_ps[:], lhsT=ones[:], rhs=bias_row[:], start=True, stop=True)
+            nc.scalar.copy(out=bias_all[:], in_=bias_ps[:])
+            return seen_by_all(part_max[:])
+
+        def softmax_exp(all_max):
+            neg_max = keep.tile([P, 1], F32)
+            nc.vector.reduce_max(out=neg_max[:], in_=all_max[:], axis=AXIS.X)
+            nc.vector.tensor_scalar_mul(out=neg_max[:], in0=neg_max[:], scalar1=-1.0)
+            part_sum = keep.tile([P, 1], F32)
+            nc.scalar.activation(
+                out=exp_cols[:], in_=logit_cols[:], func=ACT.Exp, bias=neg_max[:], scale=1.0,
+                accum_out=part_sum[:],
+            )
+            return seen_by_all(part_sum[:])
+
+        def softmax_normalise(all_sums):
+            inv_sum = keep.tile([P, 1], F32)
+            nc.vector.reduce_sum(out=inv_sum[:], in_=all_sums[:], axis=AXIS.X)
+            nc.vector.reciprocal(out=inv_sum[:], in_=inv_sum[:])
+            nc.vector.tensor_scalar_mul(out=attn[:], in0=exp_cols[:], scalar1=inv_sum[:])
+
         bias_attn = []
-        for s in range(n_tiles):
+
+        def scale_bias(s):
             scaled = keep.tile([P, CHANNELS], F32, name="bias_attn%d" % s)
             nc.vector.tensor_scalar_mul(out=scaled[:], in0=bias_all[:], scalar1=attn[:, s : s + 1])
             bias_attn.append(scaled)
 
-        feat_codes = []
-        feat_scales = []
-        for c in range(PASSES):
-            grouped = keep.tile([P, PACK, P, PACK], BF16, name="feat_grouped%d" % c, align_bytes=64)
-            for copy, first, last in ((nc.scalar.copy, 0, FEAT_SCALAR_Q), (nc.vector.tensor_copy, FEAT_SCALAR_Q, P)):
+        waiting = []
+
+        def pipeline(first_step, second_step):
+            first_step()
+            if waiting:
+                waiting.pop()()
+            waiting.append(second_step)
+
+        feat_grouped = [
+            keep.tile([P, PACK, P, PACK], BF16, name="feat_grouped%d" % c, align_bytes=64)
+            for c in range(PASSES)
+        ]
+        feat_codes = [
+            keep.tile([P, CHANNELS], U32, name="feat_codes%d" % c, align_bytes=64) for c in range(PASSES)
+        ]
+        feat_scales = [
+            keep.tile([P, CHANNELS], U8, name="feat_scales%d" % c, align_bytes=64) for c in range(PASSES)
+        ]
+
+        def regroup_features(c):
+            for copy, first, last in (
+                (nc.scalar.copy, 0, FEAT_SCALAR_Q),
+                (nc.vector.tensor_copy, FEAT_SCALAR_Q, P),
+            ):
                 copy(
-                    out=grouped[:, :, first:last, :].rearrange("p t q j -> p q j t"),
-                    in_=feat_rows[c][:, :, PACK * first : PACK * last].rearrange("p j (q t) -> p q j t", t=PACK),
+                    out=feat_grouped[c][:, :, first:last, :].rearrange("p t q j -> p q j t"),
+                    in_=feat_rows[c][:, :, PACK * first : PACK * last].rearrange(
+                        "p j (q t) -> p q j t", t=PACK
+                    ),
                 )
-            codes = keep.tile([P, CHANNELS], U32, name="feat_codes%d" % c, align_bytes=64)
-            scales = keep.tile([P, CHANNELS], U8, name="feat_scales%d" % c, align_bytes=64)
+
+        def quantise_features(c):
             nc.vector.quantize_mx(
-                out=codes[:].bitcast(FP8X4),
-                scales=scales[:],
-                in_=grouped[:].rearrange("p t q j -> p (t q j)"),
+                out=feat_codes[c][:].bitcast(FP8X4),
+                scales=feat_scales[c][:],
+                in_=feat_grouped[c][:].rearrange("p t q j -> p (t q j)"),
             )
-            feat_codes.append(codes)
-            feat_scales.append(scales)
 
-        agg_ps = [psum.tile([P, PACK, P], F32, name="agg_ps%d" % s, tag="bank") for s in range(n_tiles)]
-        for c in range(PASSES):
-            for h in range(HALVES):
-                first = h * BANK
-                grouped = keep.tile([P, BANK, PACK], BF16, name="inc_grouped%d%d" % (c, h), align_bytes=64)
-                regroup(
-                    nc.scalar.copy,
-                    grouped[:, 0:INC_SCALAR_COLS, :],
-                    inc_rows[c][:, :, first : first + INC_SCALAR_COLS],
-                )
-                regroup(
-                    nc.vector.tensor_copy,
-                    grouped[:, INC_SCALAR_COLS:BANK, :],
-                    inc_rows[c][:, :, first + INC_SCALAR_COLS : first + BANK],
-                )
-                codes = keep.tile([P, BANK], U32, name="inc_codes%d%d" % (c, h), align_bytes=64)
-                scales = keep.tile([P, BANK], U8, name="inc_scales%d%d" % (c, h), align_bytes=64)
-                nc.vector.quantize_mx(
-                    out=codes[:].bitcast(FP8X4),
-                    scales=scales[:],
-                    in_=grouped[:].rearrange("p e j -> p (e j)"),
-                )
-                for i in range(TILES):
-                    for t in range(PACK):
-                        nc.tensor.matmul_mx(
-                            out=agg_ps[h * TILES + i][:, t, :],
-                            lhsT=feat_codes[c][:, t * P : (t + 1) * P].bitcast(FP8X4),
-                            lhsT_scale=feat_scales[c][:, t * P : (t + 1) * P],
-                            rhs=codes[:, i * P : (i + 1) * P].bitcast(FP8X4),
-                            rhs_scale=scales[:, i * P : (i + 1) * P],
-                            start=(c == 0 and t == 0),
-                            stop=(c == PASSES - 1 and t == PACK - 1),
-                        )
+        def tiles_by_pass_and_half(shape, dtype, name):
+            return [
+                [keep.tile(shape, dtype, name="%s%d%d" % (name, c, h), align_bytes=64) for h in range(HALVES)]
+                for c in range(PASSES)
+            ]
 
-        for s in range(n_tiles):
+        inc_grouped = tiles_by_pass_and_half([P, BANK, PACK], BF16, "inc_grouped")
+        inc_codes = tiles_by_pass_and_half([P, BANK], U32, "inc_codes")
+        inc_scales = tiles_by_pass_and_half([P, BANK], U8, "inc_scales")
+
+        def regroup_incidence(c, h):
+            for copy, first, last in (
+                (nc.scalar.copy, 0, INC_SCALAR_COLS),
+                (nc.vector.tensor_copy, INC_SCALAR_COLS, BANK),
+            ):
+                copy(
+                    out=inc_grouped[c][h][:, first:last, :].rearrange("p (g i) j -> p g j i", i=RUN),
+                    in_=inc_rows[c][:, :, h * BANK + first : h * BANK + last].rearrange(
+                        "p j (g i) -> p g j i", i=RUN
+                    ),
+                )
+
+        agg_ps = []
+
+        def quantise_incidence_and_multiply(c, h):
+            nc.vector.quantize_mx(
+                out=inc_codes[c][h][:].bitcast(FP8X4),
+                scales=inc_scales[c][h][:],
+                in_=inc_grouped[c][h][:].rearrange("p e j -> p (e j)"),
+            )
+            for i in range(BANK // P):
+                s = h * BANK // P + i
+                if c == 0:
+                    agg_ps.append(psum.tile([P, PACK, P], F32, name="agg_ps%d" % s, tag="bank"))
+                for t in range(PACK):
+                    nc.tensor.matmul_mx(
+                        out=agg_ps[s][:, t, :],
+                        lhsT=feat_codes[c][:, t * P : (t + 1) * P].bitcast(FP8X4),
+                        lhsT_scale=feat_scales[c][:, t * P : (t + 1) * P],
+                        rhs=inc_codes[c][h][:, i * P : (i + 1) * P].bitcast(FP8X4),
+                        rhs_scale=inc_scales[c][h][:, i * P : (i + 1) * P],
+                        start=(c == 0 and t == 0),
+                        stop=(c == PASSES - 1 and t == PACK - 1),
+                    )
+
+        lin_ps = []
+
+        def quantise_agg_and_multiply(s):
             agg_grouped = keep.tile([P, P, PACK], BF16, name="agg_grouped%d" % s, align_bytes=64)
             nc.scalar.copy(out=agg_grouped[:], in_=agg_ps[s][:].rearrange("p t e -> p e t"))
             agg_codes = keep.tile([P, P], U32, name="agg_codes%d" % s, align_bytes=64)
@@ -191,7 +231,7 @@ def tile_heterogeneoustemporalhypergraphnn_pa_kernel(
                 scales=agg_scales[:],
                 in_=agg_grouped[:].rearrange("p e t -> p (e t)"),
             )
-            lin = psum.tile([P, CHANNELS], F32, name="lin", tag="bank")
+            lin = psum.tile([P, CHANNELS], F32, name="lin%d" % s, tag="bank")
             nc.tensor.matmul_mx(
                 out=lin[:],
                 lhsT=agg_codes[:].bitcast(FP8X4),
@@ -201,9 +241,33 @@ def tile_heterogeneoustemporalhypergraphnn_pa_kernel(
                 start=True,
                 stop=True,
             )
+            lin_ps.append(lin)
+
+        def finish(s):
             result = keep.tile([P, CHANNELS], F32, name="result%d" % s)
             nc.vector.scalar_tensor_tensor(
-                out=result[:], in0=lin[:], scalar=attn[:, s : s + 1], in1=bias_attn[s][:],
+                out=result[:], in0=lin_ps[s][:], scalar=attn[:, s : s + 1], in1=bias_attn[s][:],
                 op0=ALU.mult, op1=ALU.add,
             )
             nc.sync.dma_start(out=out[s * P : (s + 1) * P, :], in_=result[:])
+
+        def features(c):
+            pipeline(lambda: regroup_features(c), lambda: quantise_features(c))
+
+        all_max = softmax_partition_max()
+        features(0)
+        all_sums = softmax_exp(all_max)
+        features(1)
+        softmax_normalise(all_sums)
+        for c in range(PASSES):
+            for h in range(HALVES):
+                pipeline(
+                    lambda: regroup_incidence(c, h), lambda c=c, h=h: quantise_incidence_and_multiply(c, h)
+                )
+                scale_bias(c * HALVES + h)
+            if c + 2 < PASSES:
+                features(c + 2)
+        waiting.pop()()
+        for s in range(TILES):
+            pipeline(lambda: quantise_agg_and_multiply(s), lambda s=s: finish(s))
+        waiting.pop()()

@@ -26,8 +26,9 @@ HALVES = EDGES // BANK
 TILES = EDGES // P
 RUN = 4
 
-INC_SCALAR_COLS = 320
+INC_SCALAR_COLS = 304
 FEAT_SCALAR_Q = 64
+EARLY_BIAS_TILES = 4
 
 FLOPS = 2 * NODES * EDGES * CHANNELS + 2 * EDGES * CHANNELS * CHANNELS
 
@@ -138,11 +139,15 @@ def tile_heterogeneoustemporalhypergraphnn_pa_kernel(
 
         waiting = []
 
-        def pipeline(first_step, second_step):
+        def pipeline(first_step, second_step, ahead):
             first_step()
-            if waiting:
-                waiting.pop()()
             waiting.append(second_step)
+            if len(waiting) > ahead:
+                waiting.pop(0)()
+
+        def drain():
+            while waiting:
+                waiting.pop(0)()
 
         feat_grouped = [
             keep.tile([P, PACK, P, PACK], BF16, name="feat_grouped%d" % c, align_bytes=64)
@@ -252,7 +257,7 @@ def tile_heterogeneoustemporalhypergraphnn_pa_kernel(
             nc.sync.dma_start(out=out[s * P : (s + 1) * P, :], in_=result[:])
 
         def features(c):
-            pipeline(lambda: regroup_features(c), lambda: quantise_features(c))
+            pipeline(lambda: regroup_features(c), lambda: quantise_features(c), 1)
 
         all_max = softmax_partition_max()
         features(0)
@@ -262,12 +267,18 @@ def tile_heterogeneoustemporalhypergraphnn_pa_kernel(
         for c in range(PASSES):
             for h in range(HALVES):
                 pipeline(
-                    lambda: regroup_incidence(c, h), lambda c=c, h=h: quantise_incidence_and_multiply(c, h)
+                    lambda: regroup_incidence(c, h),
+                    lambda c=c, h=h: quantise_incidence_and_multiply(c, h),
+                    1,
                 )
-                scale_bias(c * HALVES + h)
+                if len(bias_attn) < EARLY_BIAS_TILES:
+                    scale_bias(len(bias_attn))
             if c + 2 < PASSES:
                 features(c + 2)
-        waiting.pop()()
+        drain()
         for s in range(TILES):
-            pipeline(lambda: quantise_agg_and_multiply(s), lambda s=s: finish(s))
-        waiting.pop()()
+            pipeline(lambda: quantise_agg_and_multiply(s), lambda s=s: finish(s), 2)
+            for late in range(2):
+                if len(bias_attn) < TILES:
+                    scale_bias(len(bias_attn))
+        drain()

@@ -22,13 +22,14 @@ NODES = 2048
 EDGES = 1024
 CHANNELS = 512
 PASSES = NODES // K_PASS
-HALVES = EDGES // BANK
 TILES = EDGES // P
 RUN = 4
 
-INC_SCALAR_COLS = 304
-FEAT_SCALAR_Q = 64
-EARLY_BIAS_TILES = 4
+GROUPS = ((0, 512), (512, 768), (768, 1024))
+LOAD = 512
+
+INC_SCALAR_COLS = ((512, 512, 512, 384), (256, 256, 256, 256), (256, 256, 256, 0))
+FEAT_SCALAR_Q = (64, 0, 0, 0)
 
 FLOPS = 2 * NODES * EDGES * CHANNELS + 2 * EDGES * CHANNELS * CHANNELS
 
@@ -42,15 +43,34 @@ def tile_heterogeneoustemporalhypergraphnn_pa_kernel(
         psum = ctx.enter_context(tc.psum_pool(name="psum", bufs=8))
         ctx.enter_context(tc.manual_schedule())
 
-        def load_pass(source, c, width, name):
-            rows = keep.tile([P, PACK, width], BF16, name="%s%d" % (name, c))
-            nc.sync.dma_start(
-                out=rows[:],
-                in_=source[c * K_PASS : (c + 1) * K_PASS, :].rearrange("(p j) w -> p j w", j=PACK),
-            )
-            return rows
+        warm = keep.tile([P, 1], F32)
+        nc.vector.memset(warm[:], 0.0)
+        nc.scalar.activation(out=warm[:], in_=warm[:], func=ACT.Exp)
 
-        feat_rows = [load_pass(node_features, 0, CHANNELS, "feat_rows")]
+        feat_rows = [keep.tile([P, PACK, CHANNELS], BF16, name="feat_rows%d" % c) for c in range(PASSES)]
+        inc_rows = [
+            [keep.tile([P, PACK, LOAD], BF16, name="inc_rows%d%d" % (c, h)) for h in range(EDGES // LOAD)]
+            for c in range(PASSES)
+        ]
+
+        def load_features(c, first, last):
+            nc.sync.dma_start(
+                out=feat_rows[c][:, :, first:last],
+                in_=node_features[c * K_PASS : (c + 1) * K_PASS, first:last].rearrange(
+                    "(p j) w -> p j w", j=PACK
+                ),
+            )
+
+        def load_incidence(c, h):
+            nc.sync.dma_start(
+                out=inc_rows[c][h][:],
+                in_=incidence[c * K_PASS : (c + 1) * K_PASS, h * LOAD : (h + 1) * LOAD].rearrange(
+                    "(p j) w -> p j w", j=PACK
+                ),
+            )
+
+        load_features(0, 0, PACK * FEAT_SCALAR_Q[0])
+        load_features(0, PACK * FEAT_SCALAR_Q[0], CHANNELS)
 
         logit_rows = keep.tile([P, P], BF16)
         nc.vector.memset(logit_rows[:], 0.0)
@@ -61,11 +81,10 @@ def tile_heterogeneoustemporalhypergraphnn_pa_kernel(
         nc.vector.memset(bias_row[:], 0.0)
         nc.sync.dma_start(out=bias_row[0:1, :], in_=b1.rearrange("(o n) -> o n", o=1))
 
-        inc_rows = []
-        for c in range(PASSES):
-            if c + 1 < PASSES:
-                feat_rows.append(load_pass(node_features, c + 1, CHANNELS, "feat_rows"))
-            inc_rows.append(load_pass(incidence, c, EDGES, "inc_rows"))
+        load_incidence(0, 0)
+        for c in range(1, PASSES):
+            load_features(c, 0, CHANNELS)
+            load_incidence(c, 0)
 
         w1_codes = keep.tile([P, CHANNELS], U32, align_bytes=64)
         nc.sync.dma_start(
@@ -79,75 +98,61 @@ def tile_heterogeneoustemporalhypergraphnn_pa_kernel(
                 out=w1_scales[32 * quadrant : 32 * quadrant + 4, :].bitcast(I32),
                 in_=W1_scales[0, 4 * quadrant : 4 * quadrant + 4, :].bitcast(I32),
             )
+        for c in range(PASSES):
+            load_incidence(c, 1)
 
         ident_bf16 = keep.tile([P, P], BF16)
         make_identity(nc, ident_bf16[:])
-        ident_f32 = keep.tile([P, P], F32)
-        make_identity(nc, ident_f32[:])
-        ones = keep.tile([P, P], BF16)
-        nc.vector.memset(ones[:], 1.0)
-        warm = keep.tile([P, 1], F32)
-        nc.vector.memset(warm[:], 0.0)
-        nc.scalar.activation(out=warm[:], in_=warm[:], func=ACT.Exp)
+        neg_ident = keep.tile([P, P], F32)
+        make_identity(nc, neg_ident[:])
+        nc.gpsimd.tensor_scalar(out=neg_ident[:], in0=neg_ident[:], scalar1=-1.0, scalar2=0.0, op0=ALU.mult, op1=ALU.add)
+        ones_bf16 = keep.tile([P, P], BF16)
+        nc.vector.memset(ones_bf16[:], 1.0)
+        ones_f32 = keep.tile([P, P], F32)
+        nc.vector.memset(ones_f32[:], 1.0)
 
-        def seen_by_all(column):
-            spread = psum.tile([P, P], F32, name="spread", tag="bank")
-            nc.tensor.matmul(
-                spread[:], lhsT=column.to_broadcast([P, P]), rhs=ident_f32[:], start=True, stop=True
-            )
-            return spread
-
-        logit_cols = keep.tile([P, TILES], F32)
         exp_cols = keep.tile([P, TILES], F32)
         attn = keep.tile([P, TILES], F32)
         bias_all = keep.tile([P, CHANNELS], F32)
 
         def softmax_partition_max():
-            logit_cols_ps = psum.tile([P, P], BF16, tag="bank")
-            nc.tensor.transpose(logit_cols_ps[:], logit_rows[:], ident_bf16[:])
-            nc.vector.tensor_copy(out=logit_cols[:], in_=logit_cols_ps[:, 0:TILES])
+            logit_cols = psum.tile([P, P], BF16, name="logit_cols", tag="bank")
+            nc.tensor.transpose(logit_cols[:], logit_rows[:], ident_bf16[:])
             part_max = keep.tile([P, 1], F32)
-            nc.vector.reduce_max(out=part_max[:], in_=logit_cols[:], axis=AXIS.X)
-            bias_ps = psum.tile([P, CHANNELS], F32, tag="bank")
-            nc.tensor.matmul(bias_ps[:], lhsT=ones[:], rhs=bias_row[:], start=True, stop=True)
-            nc.scalar.copy(out=bias_all[:], in_=bias_ps[:])
-            return seen_by_all(part_max[:])
+            nc.vector.reduce_max(out=part_max[:], in_=logit_cols[:, 0:TILES], axis=AXIS.X)
+            bias_ps = psum.tile([P, CHANNELS], F32, name="bias_ps", tag="bank")
+            nc.tensor.matmul(bias_ps[:], lhsT=ones_bf16[:], rhs=bias_row[:], start=True, stop=True)
+            neg_maxima = psum.tile([P, P], F32, name="neg_maxima", tag="bank")
+            nc.tensor.matmul(
+                neg_maxima[:], lhsT=part_max[:].to_broadcast([P, P]), rhs=neg_ident[:], start=True, stop=True
+            )
+            return logit_cols, bias_ps, neg_maxima
 
-        def softmax_exp(all_max):
+        def softmax_exp(logit_cols, bias_ps, neg_maxima):
             neg_max = keep.tile([P, 1], F32)
-            nc.vector.reduce_max(out=neg_max[:], in_=all_max[:], axis=AXIS.X)
-            nc.vector.tensor_scalar_mul(out=neg_max[:], in0=neg_max[:], scalar1=-1.0)
+            nc.vector.tensor_reduce(out=neg_max[:], in_=neg_maxima[:], axis=AXIS.X, op=ALU.min)
+            nc.vector.tensor_copy(out=bias_all[:], in_=bias_ps[:])
             part_sum = keep.tile([P, 1], F32)
             nc.scalar.activation(
-                out=exp_cols[:], in_=logit_cols[:], func=ACT.Exp, bias=neg_max[:], scale=1.0,
+                out=exp_cols[:], in_=logit_cols[:, 0:TILES], func=ACT.Exp, bias=neg_max[:], scale=1.0,
                 accum_out=part_sum[:],
             )
-            return seen_by_all(part_sum[:])
+            total = psum.tile([P, P], F32, name="total", tag="bank")
+            nc.tensor.matmul(total[:, 0:1], lhsT=ones_f32[:], rhs=part_sum[:], start=True, stop=True)
+            return total
 
-        def softmax_normalise(all_sums):
+        def softmax_normalise(total):
             inv_sum = keep.tile([P, 1], F32)
-            nc.vector.reduce_sum(out=inv_sum[:], in_=all_sums[:], axis=AXIS.X)
-            nc.vector.reciprocal(out=inv_sum[:], in_=inv_sum[:])
+            nc.vector.reciprocal(out=inv_sum[:], in_=total[:, 0:1])
             nc.vector.tensor_scalar_mul(out=attn[:], in0=exp_cols[:], scalar1=inv_sum[:])
 
         bias_attn = []
 
-        def scale_bias(s):
+        def scale_bias():
+            s = len(bias_attn)
             scaled = keep.tile([P, CHANNELS], F32, name="bias_attn%d" % s)
             nc.vector.tensor_scalar_mul(out=scaled[:], in0=bias_all[:], scalar1=attn[:, s : s + 1])
             bias_attn.append(scaled)
-
-        waiting = []
-
-        def pipeline(first_step, second_step, ahead):
-            first_step()
-            waiting.append(second_step)
-            if len(waiting) > ahead:
-                waiting.pop(0)()
-
-        def drain():
-            while waiting:
-                waiting.pop(0)()
 
         feat_grouped = [
             keep.tile([P, PACK, P, PACK], BF16, name="feat_grouped%d" % c, align_bytes=64)
@@ -162,15 +167,16 @@ def tile_heterogeneoustemporalhypergraphnn_pa_kernel(
 
         def regroup_features(c):
             for copy, first, last in (
-                (nc.scalar.copy, 0, FEAT_SCALAR_Q),
-                (nc.vector.tensor_copy, FEAT_SCALAR_Q, P),
+                (nc.scalar.copy, 0, FEAT_SCALAR_Q[c]),
+                (nc.vector.tensor_copy, FEAT_SCALAR_Q[c], P),
             ):
-                copy(
-                    out=feat_grouped[c][:, :, first:last, :].rearrange("p t q j -> p q j t"),
-                    in_=feat_rows[c][:, :, PACK * first : PACK * last].rearrange(
-                        "p j (q t) -> p q j t", t=PACK
-                    ),
-                )
+                if first < last:
+                    copy(
+                        out=feat_grouped[c][:, :, first:last, :].rearrange("p t q j -> p q j t"),
+                        in_=feat_rows[c][:, :, PACK * first : PACK * last].rearrange(
+                            "p j (q t) -> p q j t", t=PACK
+                        ),
+                    )
 
         def quantise_features(c):
             nc.vector.quantize_mx(
@@ -179,38 +185,46 @@ def tile_heterogeneoustemporalhypergraphnn_pa_kernel(
                 in_=feat_grouped[c][:].rearrange("p t q j -> p (t q j)"),
             )
 
-        def tiles_by_pass_and_half(shape, dtype, name):
+        def tiles_by_pass_and_group(shape, dtype, name):
             return [
-                [keep.tile(shape, dtype, name="%s%d%d" % (name, c, h), align_bytes=64) for h in range(HALVES)]
+                [
+                    keep.tile([P, last - first] + shape, dtype, name="%s%d%d" % (name, c, g), align_bytes=64)
+                    for g, (first, last) in enumerate(GROUPS)
+                ]
                 for c in range(PASSES)
             ]
 
-        inc_grouped = tiles_by_pass_and_half([P, BANK, PACK], BF16, "inc_grouped")
-        inc_codes = tiles_by_pass_and_half([P, BANK], U32, "inc_codes")
-        inc_scales = tiles_by_pass_and_half([P, BANK], U8, "inc_scales")
+        inc_grouped = tiles_by_pass_and_group([PACK], BF16, "inc_grouped")
+        inc_codes = tiles_by_pass_and_group([], U32, "inc_codes")
+        inc_scales = tiles_by_pass_and_group([], U8, "inc_scales")
 
-        def regroup_incidence(c, h):
+        def regroup_incidence(c, g):
+            start, end = GROUPS[g]
+            cut = INC_SCALAR_COLS[g][c]
             for copy, first, last in (
-                (nc.scalar.copy, 0, INC_SCALAR_COLS),
-                (nc.vector.tensor_copy, INC_SCALAR_COLS, BANK),
+                (nc.scalar.copy, 0, cut),
+                (nc.vector.tensor_copy, cut, end - start),
             ):
-                copy(
-                    out=inc_grouped[c][h][:, first:last, :].rearrange("p (g i) j -> p g j i", i=RUN),
-                    in_=inc_rows[c][:, :, h * BANK + first : h * BANK + last].rearrange(
-                        "p j (g i) -> p g j i", i=RUN
-                    ),
-                )
+                if first < last:
+                    offset = start % LOAD
+                    copy(
+                        out=inc_grouped[c][g][:, first:last, :].rearrange("p (g i) j -> p g j i", i=RUN),
+                        in_=inc_rows[c][start // LOAD][:, :, offset + first : offset + last].rearrange(
+                            "p j (g i) -> p g j i", i=RUN
+                        ),
+                    )
 
         agg_ps = []
 
-        def quantise_incidence_and_multiply(c, h):
+        def quantise_incidence_and_multiply(c, g):
             nc.vector.quantize_mx(
-                out=inc_codes[c][h][:].bitcast(FP8X4),
-                scales=inc_scales[c][h][:],
-                in_=inc_grouped[c][h][:].rearrange("p e j -> p (e j)"),
+                out=inc_codes[c][g][:].bitcast(FP8X4),
+                scales=inc_scales[c][g][:],
+                in_=inc_grouped[c][g][:].rearrange("p e j -> p (e j)"),
             )
-            for i in range(BANK // P):
-                s = h * BANK // P + i
+            start, end = GROUPS[g]
+            for i in range((end - start) // P):
+                s = start // P + i
                 if c == 0:
                     agg_ps.append(psum.tile([P, PACK, P], F32, name="agg_ps%d" % s, tag="bank"))
                 for t in range(PACK):
@@ -218,23 +232,27 @@ def tile_heterogeneoustemporalhypergraphnn_pa_kernel(
                         out=agg_ps[s][:, t, :],
                         lhsT=feat_codes[c][:, t * P : (t + 1) * P].bitcast(FP8X4),
                         lhsT_scale=feat_scales[c][:, t * P : (t + 1) * P],
-                        rhs=inc_codes[c][h][:, i * P : (i + 1) * P].bitcast(FP8X4),
-                        rhs_scale=inc_scales[c][h][:, i * P : (i + 1) * P],
+                        rhs=inc_codes[c][g][:, i * P : (i + 1) * P].bitcast(FP8X4),
+                        rhs_scale=inc_scales[c][g][:, i * P : (i + 1) * P],
                         start=(c == 0 and t == 0),
                         stop=(c == PASSES - 1 and t == PACK - 1),
                     )
 
+        agg_grouped = [
+            keep.tile([P, P, PACK], BF16, name="agg_grouped%d" % s, align_bytes=64) for s in range(TILES)
+        ]
         lin_ps = []
 
+        def agg_out(s, copy):
+            copy(out=agg_grouped[s][:], in_=agg_ps[s][:].rearrange("p t e -> p e t"))
+
         def quantise_agg_and_multiply(s):
-            agg_grouped = keep.tile([P, P, PACK], BF16, name="agg_grouped%d" % s, align_bytes=64)
-            nc.scalar.copy(out=agg_grouped[:], in_=agg_ps[s][:].rearrange("p t e -> p e t"))
             agg_codes = keep.tile([P, P], U32, name="agg_codes%d" % s, align_bytes=64)
             agg_scales = keep.tile([P, P], U8, name="agg_scales%d" % s, align_bytes=64)
             nc.vector.quantize_mx(
                 out=agg_codes[:].bitcast(FP8X4),
                 scales=agg_scales[:],
-                in_=agg_grouped[:].rearrange("p e t -> p (e t)"),
+                in_=agg_grouped[s][:].rearrange("p e t -> p (e t)"),
             )
             lin = psum.tile([P, CHANNELS], F32, name="lin%d" % s, tag="bank")
             nc.tensor.matmul_mx(
@@ -256,29 +274,42 @@ def tile_heterogeneoustemporalhypergraphnn_pa_kernel(
             )
             nc.sync.dma_start(out=out[s * P : (s + 1) * P, :], in_=result[:])
 
-        def features(c):
-            pipeline(lambda: regroup_features(c), lambda: quantise_features(c), 1)
+        regroup_features(0)
+        softmax = softmax_partition_max()
+        regroup_incidence(0, 0)
+        quantise_features(0)
+        softmax = softmax_exp(*softmax)
+        regroup_features(1)
+        softmax_normalise(softmax)
+        quantise_incidence_and_multiply(0, 0)
+        for c in range(1, PASSES):
+            regroup_incidence(c, 0)
+            quantise_features(c)
+            if c + 1 < PASSES:
+                regroup_features(c + 1)
+                quantise_incidence_and_multiply(c, 0)
+            else:
+                scale_bias()
 
-        all_max = softmax_partition_max()
-        features(0)
-        all_sums = softmax_exp(all_max)
-        features(1)
-        softmax_normalise(all_sums)
-        for c in range(PASSES):
-            for h in range(HALVES):
-                pipeline(
-                    lambda: regroup_incidence(c, h),
-                    lambda c=c, h=h: quantise_incidence_and_multiply(c, h),
-                    1,
-                )
-                if len(bias_attn) < EARLY_BIAS_TILES:
-                    scale_bias(len(bias_attn))
-            if c + 2 < PASSES:
-                features(c + 2)
-        drain()
-        for s in range(TILES):
-            pipeline(lambda: quantise_agg_and_multiply(s), lambda s=s: finish(s), 2)
-            for late in range(2):
-                if len(bias_attn) < TILES:
-                    scale_bias(len(bias_attn))
-        drain()
+        pieces = [(c, g) for g in (1, 2) for c in range(PASSES)]
+        before = (PASSES - 1, 0)
+        for step, piece in enumerate(pieces):
+            regroup_incidence(*piece)
+            quantise_incidence_and_multiply(*before)
+            before = piece
+            if len(bias_attn) < TILES:
+                scale_bias()
+            if 1 <= step < 7:
+                agg_out(step - 1, nc.scalar.copy)
+            if 2 <= step < 8:
+                quantise_agg_and_multiply(step - 2)
+            if 3 <= step:
+                finish(step - 3)
+        quantise_incidence_and_multiply(*before)
+        agg_out(6, nc.scalar.copy)
+        finish(5)
+        agg_out(7, nc.scalar.copy)
+        quantise_agg_and_multiply(6)
+        quantise_agg_and_multiply(7)
+        finish(6)
+        finish(7)

@@ -25,11 +25,11 @@ PASSES = NODES // K_PASS
 TILES = EDGES // P
 RUN = 4
 
-GROUPS = ((0, 512), (512, 768), (768, 1024))
-LOAD = 512
+SPLIT_FROM = 2
+HALF = 512
 
-INC_SCALAR_COLS = ((512, 512, 512, 384), (256, 256, 256, 256), (256, 256, 256, 0))
-FEAT_SCALAR_Q = (64, 0, 0, 0)
+FEAT_SCALAR_Q = 64
+INC_SCALAR_SHARE = 0.59375
 
 FLOPS = 2 * NODES * EDGES * CHANNELS + 2 * EDGES * CHANNELS * CHANNELS
 
@@ -48,29 +48,16 @@ def tile_heterogeneoustemporalhypergraphnn_pa_kernel(
         nc.scalar.activation(out=warm[:], in_=warm[:], func=ACT.Exp)
 
         feat_rows = [keep.tile([P, PACK, CHANNELS], BF16, name="feat_rows%d" % c) for c in range(PASSES)]
-        inc_rows = [
-            [keep.tile([P, PACK, LOAD], BF16, name="inc_rows%d%d" % (c, h)) for h in range(EDGES // LOAD)]
-            for c in range(PASSES)
-        ]
+        inc_rows = [keep.tile([P, PACK, EDGES], BF16, name="inc_rows%d" % c) for c in range(PASSES)]
 
-        def load_features(c, first, last):
+        def load(rows, source, c, first, last):
             nc.sync.dma_start(
-                out=feat_rows[c][:, :, first:last],
-                in_=node_features[c * K_PASS : (c + 1) * K_PASS, first:last].rearrange(
-                    "(p j) w -> p j w", j=PACK
-                ),
+                out=rows[c][:, :, first:last],
+                in_=source[c * K_PASS : (c + 1) * K_PASS, first:last].rearrange("(p j) w -> p j w", j=PACK),
             )
 
-        def load_incidence(c, h):
-            nc.sync.dma_start(
-                out=inc_rows[c][h][:],
-                in_=incidence[c * K_PASS : (c + 1) * K_PASS, h * LOAD : (h + 1) * LOAD].rearrange(
-                    "(p j) w -> p j w", j=PACK
-                ),
-            )
-
-        load_features(0, 0, PACK * FEAT_SCALAR_Q[0])
-        load_features(0, PACK * FEAT_SCALAR_Q[0], CHANNELS)
+        load(feat_rows, node_features, 0, 0, PACK * FEAT_SCALAR_Q)
+        load(feat_rows, node_features, 0, PACK * FEAT_SCALAR_Q, CHANNELS)
 
         logit_rows = keep.tile([P, P], BF16)
         nc.vector.memset(logit_rows[:], 0.0)
@@ -81,10 +68,14 @@ def tile_heterogeneoustemporalhypergraphnn_pa_kernel(
         nc.vector.memset(bias_row[:], 0.0)
         nc.sync.dma_start(out=bias_row[0:1, :], in_=b1.rearrange("(o n) -> o n", o=1))
 
-        load_incidence(0, 0)
-        for c in range(1, PASSES):
-            load_features(c, 0, CHANNELS)
-            load_incidence(c, 0)
+        load(inc_rows, incidence, 0, 0, HALF)
+        load(inc_rows, incidence, 0, HALF, EDGES)
+        load(feat_rows, node_features, 1, 0, CHANNELS)
+        load(inc_rows, incidence, 1, 0, EDGES)
+        for c in range(SPLIT_FROM, PASSES):
+            load(feat_rows, node_features, c, 0, CHANNELS)
+        for c in range(SPLIT_FROM, PASSES):
+            load(inc_rows, incidence, c, 0, HALF)
 
         w1_codes = keep.tile([P, CHANNELS], U32, align_bytes=64)
         nc.sync.dma_start(
@@ -98,8 +89,8 @@ def tile_heterogeneoustemporalhypergraphnn_pa_kernel(
                 out=w1_scales[32 * quadrant : 32 * quadrant + 4, :].bitcast(I32),
                 in_=W1_scales[0, 4 * quadrant : 4 * quadrant + 4, :].bitcast(I32),
             )
-        for c in range(PASSES):
-            load_incidence(c, 1)
+        for c in range(SPLIT_FROM, PASSES):
+            load(inc_rows, incidence, c, HALF, EDGES)
 
         ident_bf16 = keep.tile([P, P], BF16)
         make_identity(nc, ident_bf16[:])
@@ -167,16 +158,15 @@ def tile_heterogeneoustemporalhypergraphnn_pa_kernel(
 
         def regroup_features(c):
             for copy, first, last in (
-                (nc.scalar.copy, 0, FEAT_SCALAR_Q[c]),
-                (nc.vector.tensor_copy, FEAT_SCALAR_Q[c], P),
+                (nc.scalar.copy, 0, FEAT_SCALAR_Q),
+                (nc.vector.tensor_copy, FEAT_SCALAR_Q, P),
             ):
-                if first < last:
-                    copy(
-                        out=feat_grouped[c][:, :, first:last, :].rearrange("p t q j -> p q j t"),
-                        in_=feat_rows[c][:, :, PACK * first : PACK * last].rearrange(
-                            "p j (q t) -> p q j t", t=PACK
-                        ),
-                    )
+                copy(
+                    out=feat_grouped[c][:, :, first:last, :].rearrange("p t q j -> p q j t"),
+                    in_=feat_rows[c][:, :, PACK * first : PACK * last].rearrange(
+                        "p j (q t) -> p q j t", t=PACK
+                    ),
+                )
 
         def quantise_features(c):
             nc.vector.quantize_mx(
@@ -185,46 +175,29 @@ def tile_heterogeneoustemporalhypergraphnn_pa_kernel(
                 in_=feat_grouped[c][:].rearrange("p t q j -> p (t q j)"),
             )
 
-        def tiles_by_pass_and_group(shape, dtype, name):
-            return [
-                [
-                    keep.tile([P, last - first] + shape, dtype, name="%s%d%d" % (name, c, g), align_bytes=64)
-                    for g, (first, last) in enumerate(GROUPS)
-                ]
-                for c in range(PASSES)
-            ]
+        inc_grouped = [
+            keep.tile([P, EDGES, PACK], BF16, name="inc_grouped%d" % c, align_bytes=64) for c in range(PASSES)
+        ]
+        inc_codes = [keep.tile([P, EDGES], U32, name="inc_codes%d" % c, align_bytes=64) for c in range(PASSES)]
+        inc_scales = [keep.tile([P, EDGES], U8, name="inc_scales%d" % c, align_bytes=64) for c in range(PASSES)]
 
-        inc_grouped = tiles_by_pass_and_group([PACK], BF16, "inc_grouped")
-        inc_codes = tiles_by_pass_and_group([], U32, "inc_codes")
-        inc_scales = tiles_by_pass_and_group([], U8, "inc_scales")
-
-        def regroup_incidence(c, g):
-            start, end = GROUPS[g]
-            cut = INC_SCALAR_COLS[g][c]
-            for copy, first, last in (
-                (nc.scalar.copy, 0, cut),
-                (nc.vector.tensor_copy, cut, end - start),
-            ):
-                if first < last:
-                    offset = start % LOAD
-                    copy(
-                        out=inc_grouped[c][g][:, first:last, :].rearrange("p (g i) j -> p g j i", i=RUN),
-                        in_=inc_rows[c][start // LOAD][:, :, offset + first : offset + last].rearrange(
-                            "p j (g i) -> p g j i", i=RUN
-                        ),
-                    )
+        def regroup_incidence(c, start, end):
+            cut = start + int((end - start) * INC_SCALAR_SHARE) // 16 * 16
+            for copy, first, last in ((nc.scalar.copy, start, cut), (nc.vector.tensor_copy, cut, end)):
+                copy(
+                    out=inc_grouped[c][:, first:last, :].rearrange("p (g i) j -> p g j i", i=RUN),
+                    in_=inc_rows[c][:, :, first:last].rearrange("p j (g i) -> p g j i", i=RUN),
+                )
 
         agg_ps = []
 
-        def quantise_incidence_and_multiply(c, g):
+        def quantise_incidence_and_multiply(c, start, end):
             nc.vector.quantize_mx(
-                out=inc_codes[c][g][:].bitcast(FP8X4),
-                scales=inc_scales[c][g][:],
-                in_=inc_grouped[c][g][:].rearrange("p e j -> p (e j)"),
+                out=inc_codes[c][:, start:end].bitcast(FP8X4),
+                scales=inc_scales[c][:, start:end],
+                in_=inc_grouped[c][:, start:end, :].rearrange("p e j -> p (e j)"),
             )
-            start, end = GROUPS[g]
-            for i in range((end - start) // P):
-                s = start // P + i
+            for s in range(start // P, end // P):
                 if c == 0:
                     agg_ps.append(psum.tile([P, PACK, P], F32, name="agg_ps%d" % s, tag="bank"))
                 for t in range(PACK):
@@ -232,8 +205,8 @@ def tile_heterogeneoustemporalhypergraphnn_pa_kernel(
                         out=agg_ps[s][:, t, :],
                         lhsT=feat_codes[c][:, t * P : (t + 1) * P].bitcast(FP8X4),
                         lhsT_scale=feat_scales[c][:, t * P : (t + 1) * P],
-                        rhs=inc_codes[c][g][:, i * P : (i + 1) * P].bitcast(FP8X4),
-                        rhs_scale=inc_scales[c][g][:, i * P : (i + 1) * P],
+                        rhs=inc_codes[c][:, s * P : (s + 1) * P].bitcast(FP8X4),
+                        rhs_scale=inc_scales[c][:, s * P : (s + 1) * P],
                         start=(c == 0 and t == 0),
                         stop=(c == PASSES - 1 and t == PACK - 1),
                     )
@@ -274,42 +247,54 @@ def tile_heterogeneoustemporalhypergraphnn_pa_kernel(
             )
             nc.sync.dma_start(out=out[s * P : (s + 1) * P, :], in_=result[:])
 
-        regroup_features(0)
-        softmax = softmax_partition_max()
-        regroup_incidence(0, 0)
-        quantise_features(0)
-        softmax = softmax_exp(*softmax)
-        regroup_features(1)
-        softmax_normalise(softmax)
-        quantise_incidence_and_multiply(0, 0)
-        for c in range(1, PASSES):
-            regroup_incidence(c, 0)
-            quantise_features(c)
-            if c + 1 < PASSES:
-                regroup_features(c + 1)
-                quantise_incidence_and_multiply(c, 0)
-            else:
-                scale_bias()
+        waiting = []
 
-        pieces = [(c, g) for g in (1, 2) for c in range(PASSES)]
-        before = (PASSES - 1, 0)
-        for step, piece in enumerate(pieces):
-            regroup_incidence(*piece)
-            quantise_incidence_and_multiply(*before)
-            before = piece
-            if len(bias_attn) < TILES:
+        def step(regroup, quantise, *piece):
+            regroup(*piece)
+            if waiting:
+                waiting.pop(0)()
+            waiting.append(lambda: quantise(*piece))
+
+        def features(c):
+            step(regroup_features, quantise_features, c)
+
+        def incidence_piece(c, start, end):
+            step(regroup_incidence, quantise_incidence_and_multiply, c, start, end)
+
+        def way_out(s):
+            if s < TILES:
+                agg_out(s, nc.scalar.copy)
+            if 1 <= s <= TILES:
+                quantise_agg_and_multiply(s - 1)
+            if 2 <= s:
+                finish(s - 2)
+
+        features(0)
+        softmax = softmax_partition_max()
+        incidence_piece(0, 0, HALF)
+        softmax = softmax_exp(*softmax)
+        incidence_piece(0, HALF, EDGES)
+        softmax_normalise(softmax)
+        features(1)
+        incidence_piece(1, 0, HALF)
+        incidence_piece(1, HALF, EDGES)
+        features(2)
+        scale_bias()
+        features(3)
+        scale_bias()
+        incidence_piece(2, 0, HALF)
+        incidence_piece(3, 0, HALF)
+        scale_bias()
+        scale_bias()
+        tiles_out = 0
+        for start, end in ((512, 768), (768, 1024)):
+            for c in range(SPLIT_FROM, PASSES):
+                incidence_piece(c, start, end)
                 scale_bias()
-            if 1 <= step < 7:
-                agg_out(step - 1, nc.scalar.copy)
-            if 2 <= step < 8:
-                quantise_agg_and_multiply(step - 2)
-            if 3 <= step:
-                finish(step - 3)
-        quantise_incidence_and_multiply(*before)
-        agg_out(6, nc.scalar.copy)
-        finish(5)
-        agg_out(7, nc.scalar.copy)
-        quantise_agg_and_multiply(6)
-        quantise_agg_and_multiply(7)
-        finish(6)
-        finish(7)
+                if (c, start) != (2, 512):
+                    way_out(tiles_out)
+                    tiles_out += 1
+        waiting.pop(0)()
+        while tiles_out < TILES + 2:
+            way_out(tiles_out)
+            tiles_out += 1

@@ -25,7 +25,6 @@ PASSES = NODES // K_PASS
 TILES = EDGES // P
 RUN = 4
 
-SPLIT_FROM = 2
 HALF = 512
 
 FEAT_SCALAR_Q = 64
@@ -47,17 +46,19 @@ def tile_heterogeneoustemporalhypergraphnn_pa_kernel(
         nc.vector.memset(warm[:], 0.0)
         nc.scalar.activation(out=warm[:], in_=warm[:], func=ACT.Exp)
 
-        feat_rows = [keep.tile([P, PACK, CHANNELS], BF16, name="feat_rows%d" % c) for c in range(PASSES)]
-        inc_rows = [keep.tile([P, PACK, EDGES], BF16, name="inc_rows%d" % c) for c in range(PASSES)]
-
-        def load(rows, source, c, first, last):
+        def load(source, c, first, last, name):
+            rows = keep.tile([P, PACK, last - first], BF16, name="%s_%d_%d" % (name, c, first))
             nc.sync.dma_start(
-                out=rows[c][:, :, first:last],
+                out=rows[:],
                 in_=source[c * K_PASS : (c + 1) * K_PASS, first:last].rearrange("(p j) w -> p j w", j=PACK),
             )
+            return rows
 
-        load(feat_rows, node_features, 0, 0, PACK * FEAT_SCALAR_Q)
-        load(feat_rows, node_features, 0, PACK * FEAT_SCALAR_Q, CHANNELS)
+        feat_rows = {}
+        inc_rows = {}
+        cut = PACK * FEAT_SCALAR_Q
+        feat_rows[0, 0] = load(node_features, 0, 0, cut, "feat")
+        feat_rows[0, cut] = load(node_features, 0, cut, CHANNELS, "feat")
 
         logit_rows = keep.tile([P, P], BF16)
         nc.vector.memset(logit_rows[:], 0.0)
@@ -68,15 +69,14 @@ def tile_heterogeneoustemporalhypergraphnn_pa_kernel(
         nc.vector.memset(bias_row[:], 0.0)
         nc.sync.dma_start(out=bias_row[0:1, :], in_=b1.rearrange("(o n) -> o n", o=1))
 
-        load(inc_rows, incidence, 0, 0, HALF)
-        load(inc_rows, incidence, 0, HALF, EDGES)
-        load(feat_rows, node_features, 1, 0, CHANNELS)
-        load(inc_rows, incidence, 1, 0, EDGES)
-        for c in range(SPLIT_FROM, PASSES):
-            load(feat_rows, node_features, c, 0, CHANNELS)
-        for c in range(SPLIT_FROM, PASSES):
-            load(inc_rows, incidence, c, 0, HALF)
-
+        feat_rows[1, 0] = load(node_features, 1, 0, CHANNELS, "feat")
+        for first in (0, HALF):
+            inc_rows[0, first] = load(incidence, 0, first, first + HALF, "inc")
+        feat_rows[2, 0] = load(node_features, 2, 0, CHANNELS, "feat")
+        inc_rows[1, 0] = load(incidence, 1, 0, EDGES, "inc")
+        feat_rows[3, 0] = load(node_features, 3, 0, CHANNELS, "feat")
+        inc_rows[2, 0] = load(incidence, 2, 0, EDGES, "inc")
+        inc_rows[3, 0] = load(incidence, 3, 0, EDGES, "inc")
         w1_codes = keep.tile([P, CHANNELS], U32, align_bytes=64)
         nc.sync.dma_start(
             out=w1_codes[:].bitcast(I32),
@@ -89,8 +89,6 @@ def tile_heterogeneoustemporalhypergraphnn_pa_kernel(
                 out=w1_scales[32 * quadrant : 32 * quadrant + 4, :].bitcast(I32),
                 in_=W1_scales[0, 4 * quadrant : 4 * quadrant + 4, :].bitcast(I32),
             )
-        for c in range(SPLIT_FROM, PASSES):
-            load(inc_rows, incidence, c, HALF, EDGES)
 
         ident_bf16 = keep.tile([P, P], BF16)
         make_identity(nc, ident_bf16[:])
@@ -156,6 +154,10 @@ def tile_heterogeneoustemporalhypergraphnn_pa_kernel(
             keep.tile([P, CHANNELS], U8, name="feat_scales%d" % c, align_bytes=64) for c in range(PASSES)
         ]
 
+        def columns(rows, c, first, last):
+            start = max(s for (k, s) in rows if k == c and s <= first)
+            return rows[c, start][:, :, first - start : last - start]
+
         def regroup_features(c):
             for copy, first, last in (
                 (nc.scalar.copy, 0, FEAT_SCALAR_Q),
@@ -163,7 +165,7 @@ def tile_heterogeneoustemporalhypergraphnn_pa_kernel(
             ):
                 copy(
                     out=feat_grouped[c][:, :, first:last, :].rearrange("p t q j -> p q j t"),
-                    in_=feat_rows[c][:, :, PACK * first : PACK * last].rearrange(
+                    in_=columns(feat_rows, c, PACK * first, PACK * last).rearrange(
                         "p j (q t) -> p q j t", t=PACK
                     ),
                 )
@@ -186,7 +188,7 @@ def tile_heterogeneoustemporalhypergraphnn_pa_kernel(
             for copy, first, last in ((nc.scalar.copy, start, cut), (nc.vector.tensor_copy, cut, end)):
                 copy(
                     out=inc_grouped[c][:, first:last, :].rearrange("p (g i) j -> p g j i", i=RUN),
-                    in_=inc_rows[c][:, :, first:last].rearrange("p j (g i) -> p g j i", i=RUN),
+                    in_=columns(inc_rows, c, first, last).rearrange("p j (g i) -> p g j i", i=RUN),
                 )
 
         agg_ps = []
@@ -271,30 +273,31 @@ def tile_heterogeneoustemporalhypergraphnn_pa_kernel(
 
         features(0)
         softmax = softmax_partition_max()
-        incidence_piece(0, 0, HALF)
-        softmax = softmax_exp(*softmax)
-        incidence_piece(0, HALF, EDGES)
-        softmax_normalise(softmax)
         features(1)
-        incidence_piece(1, 0, HALF)
-        incidence_piece(1, HALF, EDGES)
+        softmax = softmax_exp(*softmax)
+        incidence_piece(0, 0, HALF)
+        softmax_normalise(softmax)
+        incidence_piece(0, HALF, EDGES)
         features(2)
+        scale_bias()
+        incidence_piece(1, 0, HALF)
+        scale_bias()
+        incidence_piece(1, HALF, EDGES)
         scale_bias()
         features(3)
         scale_bias()
         incidence_piece(2, 0, HALF)
+        scale_bias()
+        incidence_piece(2, HALF, EDGES)
+        scale_bias()
         incidence_piece(3, 0, HALF)
+        incidence_piece(3, HALF, 768)
+        agg_out(0, nc.scalar.copy)
+        incidence_piece(3, 768, EDGES)
+        agg_out(1, nc.scalar.copy)
         scale_bias()
         scale_bias()
-        tiles_out = 0
-        for start, end in ((512, 768), (768, 1024)):
-            for c in range(SPLIT_FROM, PASSES):
-                incidence_piece(c, start, end)
-                scale_bias()
-                if (c, start) != (2, 512):
-                    way_out(tiles_out)
-                    tiles_out += 1
+        quantise_agg_and_multiply(0)
         waiting.pop(0)()
-        while tiles_out < TILES + 2:
-            way_out(tiles_out)
-            tiles_out += 1
+        for s in range(2, TILES + 2):
+            way_out(s)

@@ -56,9 +56,7 @@ def tile_heterogeneoustemporalhypergraphnn_pa_kernel(
 
         feat_rows = {}
         inc_rows = {}
-        cut = PACK * FEAT_SCALAR_Q
-        feat_rows[0, 0] = load(node_features, 0, 0, cut, "feat")
-        feat_rows[0, cut] = load(node_features, 0, cut, CHANNELS, "feat")
+        feat_rows[0, 0] = load(node_features, 0, 0, CHANNELS, "feat")
 
         logit_rows = keep.tile([P, P], BF16)
         nc.vector.memset(logit_rows[:], 0.0)
@@ -70,8 +68,7 @@ def tile_heterogeneoustemporalhypergraphnn_pa_kernel(
         nc.sync.dma_start(out=bias_row[0:1, :], in_=b1.rearrange("(o n) -> o n", o=1))
 
         feat_rows[1, 0] = load(node_features, 1, 0, CHANNELS, "feat")
-        for first in (0, HALF):
-            inc_rows[0, first] = load(incidence, 0, first, first + HALF, "inc")
+        inc_rows[0, 0] = load(incidence, 0, 0, EDGES, "inc")
         feat_rows[2, 0] = load(node_features, 2, 0, CHANNELS, "feat")
         inc_rows[1, 0] = load(incidence, 1, 0, EDGES, "inc")
         feat_rows[3, 0] = load(node_features, 3, 0, CHANNELS, "feat")

@@ -28,7 +28,7 @@ RUN = 4
 HALF = 512
 
 FEAT_SCALAR_Q = 64
-INC_SCALAR_SHARE = 0.59375
+INC_SCALAR_SHARE = 0.5625
 
 FLOPS = 2 * NODES * EDGES * CHANNELS + 2 * EDGES * CHANNELS * CHANNELS
 
@@ -139,6 +139,20 @@ def tile_heterogeneoustemporalhypergraphnn_pa_kernel(
             scaled = keep.tile([P, CHANNELS], F32, name="bias_attn%d" % s)
             nc.vector.tensor_scalar_mul(out=scaled[:], in0=bias_all[:], scalar1=attn[:, s : s + 1])
             bias_attn.append(scaled)
+
+        attn_late = keep.tile([P, TILES], F32)
+
+        def scale_bias_late():
+            s = len(bias_attn)
+            scaled = keep.tile([P, CHANNELS], F32, name="bias_attn%d" % s)
+            nc.gpsimd.tensor_scalar(
+                out=scaled[:], in0=bias_all[:], scalar1=attn_late[:, s : s + 1], scalar2=0.0,
+                op0=ALU.mult, op1=ALU.add,
+            )
+            bias_attn.append(scaled)
+
+        def release_gpsimd():
+            nc.scalar.copy(out=attn_late[:], in_=attn[:])
 
         feat_grouped = [
             keep.tile([P, PACK, P, PACK], BF16, name="feat_grouped%d" % c, align_bytes=64)
@@ -276,25 +290,45 @@ def tile_heterogeneoustemporalhypergraphnn_pa_kernel(
         softmax_normalise(softmax)
         incidence_piece(0, HALF, EDGES)
         features(2)
-        scale_bias()
         incidence_piece(1, 0, HALF)
-        scale_bias()
         incidence_piece(1, HALF, EDGES)
-        scale_bias()
         features(3)
-        scale_bias()
         incidence_piece(2, 0, HALF)
-        scale_bias()
         incidence_piece(2, HALF, EDGES)
         scale_bias()
         incidence_piece(3, 0, HALF)
+        scale_bias()
         incidence_piece(3, HALF, 768)
+        scale_bias()
         agg_out(0, nc.scalar.copy)
         incidence_piece(3, 768, EDGES)
+        release_gpsimd()
+        scale_bias_late()
+        scale_bias_late()
+        scale_bias_late()
+        scale_bias_late()
+        scale_bias_late()
         agg_out(1, nc.scalar.copy)
-        scale_bias()
-        scale_bias()
         quantise_agg_and_multiply(0)
         waiting.pop(0)()
-        for s in range(2, TILES + 2):
-            way_out(s)
+        agg_out(2, nc.scalar.copy)
+        quantise_agg_and_multiply(1)
+        finish(0)
+        agg_out(3, nc.scalar.copy)
+        quantise_agg_and_multiply(2)
+        finish(1)
+        agg_out(4, nc.scalar.copy)
+        quantise_agg_and_multiply(3)
+        finish(2)
+        agg_out(5, nc.scalar.copy)
+        quantise_agg_and_multiply(4)
+        finish(3)
+        agg_out(6, nc.scalar.copy)
+        quantise_agg_and_multiply(5)
+        finish(4)
+        agg_out(7, nc.scalar.copy)
+        quantise_agg_and_multiply(6)
+        finish(5)
+        quantise_agg_and_multiply(7)
+        finish(6)
+        finish(7)

@@ -28,7 +28,7 @@ RUN = 4
 HALF = 512
 
 FEAT_SCALAR_Q = 64
-INC_SCALAR_SHARE = 0.5625
+INC_SCALAR_SHARE = 0.53125
 
 FLOPS = 2 * NODES * EDGES * CHANNELS + 2 * EDGES * CHANNELS * CHANNELS
 
@@ -68,7 +68,8 @@ def tile_heterogeneoustemporalhypergraphnn_pa_kernel(
         nc.sync.dma_start(out=bias_row[0:1, :], in_=b1.rearrange("(o n) -> o n", o=1))
 
         feat_rows[1, 0] = load(node_features, 1, 0, CHANNELS, "feat")
-        inc_rows[0, 0] = load(incidence, 0, 0, EDGES, "inc")
+        for first in (0, HALF):
+            inc_rows[0, first] = load(incidence, 0, first, first + HALF, "inc")
         feat_rows[2, 0] = load(node_features, 2, 0, CHANNELS, "feat")
         inc_rows[1, 0] = load(incidence, 1, 0, EDGES, "inc")
         feat_rows[3, 0] = load(node_features, 3, 0, CHANNELS, "feat")
@@ -117,7 +118,7 @@ def tile_heterogeneoustemporalhypergraphnn_pa_kernel(
         def softmax_exp(logit_cols, bias_ps, neg_maxima):
             neg_max = keep.tile([P, 1], F32)
             nc.vector.tensor_reduce(out=neg_max[:], in_=neg_maxima[:], axis=AXIS.X, op=ALU.min)
-            nc.vector.tensor_copy(out=bias_all[:], in_=bias_ps[:])
+            nc.scalar.copy(out=bias_all[:], in_=bias_ps[:])
             part_sum = keep.tile([P, 1], F32)
             nc.scalar.activation(
                 out=exp_cols[:], in_=logit_cols[:, 0:TILES], func=ACT.Exp, bias=neg_max[:], scale=1.0,
@@ -295,19 +296,19 @@ def tile_heterogeneoustemporalhypergraphnn_pa_kernel(
         features(3)
         incidence_piece(2, 0, HALF)
         incidence_piece(2, HALF, EDGES)
-        scale_bias()
         incidence_piece(3, 0, HALF)
-        scale_bias()
         incidence_piece(3, HALF, 768)
-        scale_bias()
-        agg_out(0, nc.scalar.copy)
-        incidence_piece(3, 768, EDGES)
         release_gpsimd()
         scale_bias_late()
         scale_bias_late()
         scale_bias_late()
         scale_bias_late()
         scale_bias_late()
+        scale_bias_late()
+        scale_bias_late()
+        scale_bias_late()
+        agg_out(0, nc.scalar.copy)
+        incidence_piece(3, 768, EDGES)
         agg_out(1, nc.scalar.copy)
         quantise_agg_and_multiply(0)
         waiting.pop(0)()

@@ -67,26 +67,33 @@ def tile_heterogeneoustemporalhypergraphnn_pa_kernel(
         nc.vector.memset(bias_row[:], 0.0)
         nc.sync.dma_start(out=bias_row[0:1, :], in_=b1.rearrange("(o n) -> o n", o=1))
 
-        feat_rows[1, 0] = load(node_features, 1, 0, CHANNELS, "feat")
-        for first in (0, HALF):
-            inc_rows[0, first] = load(incidence, 0, first, first + HALF, "inc")
-        feat_rows[2, 0] = load(node_features, 2, 0, CHANNELS, "feat")
-        inc_rows[1, 0] = load(incidence, 1, 0, EDGES, "inc")
-        feat_rows[3, 0] = load(node_features, 3, 0, CHANNELS, "feat")
-        inc_rows[2, 0] = load(incidence, 2, 0, EDGES, "inc")
-        inc_rows[3, 0] = load(incidence, 3, 0, EDGES, "inc")
         w1_codes = keep.tile([P, CHANNELS], U32, align_bytes=64)
-        nc.sync.dma_start(
-            out=w1_codes[:].bitcast(I32),
-            in_=W1_words[0].rearrange("p n t -> p (n t)").bitcast(I32),
-        )
         w1_scales = keep.tile([P, CHANNELS], U8, align_bytes=64)
         nc.vector.memset(w1_scales[:].bitcast(I32), 0)
-        for quadrant in range(4):
+
+        def load_w1():
             nc.sync.dma_start(
-                out=w1_scales[32 * quadrant : 32 * quadrant + 4, :].bitcast(I32),
-                in_=W1_scales[0, 4 * quadrant : 4 * quadrant + 4, :].bitcast(I32),
+                out=w1_codes[:].bitcast(I32),
+                in_=W1_words[0].rearrange("p n t -> p (n t)").bitcast(I32),
             )
+            for quadrant in range(4):
+                nc.sync.dma_start(
+                    out=w1_scales[32 * quadrant : 32 * quadrant + 4, :].bitcast(I32),
+                    in_=W1_scales[0, 4 * quadrant : 4 * quadrant + 4, :].bitcast(I32),
+                )
+
+        feat_rows[1, 0] = load(node_features, 1, 0, CHANNELS, "feat")
+        inc_rows[0, 0] = load(incidence, 0, 0, HALF, "inc")
+        feat_rows[2, 0] = load(node_features, 2, 0, CHANNELS, "feat")
+        inc_rows[1, 0] = load(incidence, 1, 0, HALF, "inc")
+        feat_rows[3, 0] = load(node_features, 3, 0, CHANNELS, "feat")
+        inc_rows[2, 0] = load(incidence, 2, 0, HALF, "inc")
+        inc_rows[3, 0] = load(incidence, 3, 0, HALF, "inc")
+        inc_rows[0, HALF] = load(incidence, 0, HALF, EDGES, "inc")
+        load_w1()
+        inc_rows[1, HALF] = load(incidence, 1, HALF, EDGES, "inc")
+        inc_rows[2, HALF] = load(incidence, 2, HALF, EDGES, "inc")
+        inc_rows[3, HALF] = load(incidence, 3, HALF, EDGES, "inc")
 
         ident_bf16 = keep.tile([P, P], BF16)
         make_identity(nc, ident_bf16[:])
@@ -289,15 +296,12 @@ def tile_heterogeneoustemporalhypergraphnn_pa_kernel(
         softmax = softmax_exp(*softmax)
         incidence_piece(0, 0, HALF)
         softmax_normalise(softmax)
-        incidence_piece(0, HALF, EDGES)
         features(2)
         incidence_piece(1, 0, HALF)
-        incidence_piece(1, HALF, EDGES)
         features(3)
         incidence_piece(2, 0, HALF)
-        incidence_piece(2, HALF, EDGES)
         incidence_piece(3, 0, HALF)
-        incidence_piece(3, HALF, 768)
+        incidence_piece(0, HALF, EDGES)
         release_gpsimd()
         scale_bias_late()
         scale_bias_late()
@@ -308,18 +312,21 @@ def tile_heterogeneoustemporalhypergraphnn_pa_kernel(
         scale_bias_late()
         scale_bias_late()
         agg_out(0, nc.scalar.copy)
-        incidence_piece(3, 768, EDGES)
+        incidence_piece(1, HALF, EDGES)
         agg_out(1, nc.scalar.copy)
         quantise_agg_and_multiply(0)
-        waiting.pop(0)()
+        incidence_piece(2, HALF, EDGES)
         agg_out(2, nc.scalar.copy)
         quantise_agg_and_multiply(1)
         finish(0)
+        incidence_piece(3, 512, 768)
         agg_out(3, nc.scalar.copy)
         quantise_agg_and_multiply(2)
         finish(1)
-        agg_out(4, nc.scalar.copy)
+        incidence_piece(3, 768, 1024)
         quantise_agg_and_multiply(3)
+        waiting.pop(0)()
+        agg_out(4, nc.scalar.copy)
         finish(2)
         agg_out(5, nc.scalar.copy)
         quantise_agg_and_multiply(4)

@@ -82,12 +82,12 @@ def tile_heterogeneoustemporalhypergraphnn_pa_kernel(
                     in_=W1_scales[0, 4 * quadrant : 4 * quadrant + 4, :].bitcast(I32),
                 )
 
-        feat_rows[1, 0] = load(node_features, 1, 0, CHANNELS, "feat")
         inc_rows[0, 0] = load(incidence, 0, 0, HALF, "inc")
-        feat_rows[2, 0] = load(node_features, 2, 0, CHANNELS, "feat")
+        feat_rows[1, 0] = load(node_features, 1, 0, CHANNELS, "feat")
         inc_rows[1, 0] = load(incidence, 1, 0, HALF, "inc")
-        feat_rows[3, 0] = load(node_features, 3, 0, CHANNELS, "feat")
+        feat_rows[2, 0] = load(node_features, 2, 0, CHANNELS, "feat")
         inc_rows[2, 0] = load(incidence, 2, 0, HALF, "inc")
+        feat_rows[3, 0] = load(node_features, 3, 0, CHANNELS, "feat")
         inc_rows[3, 0] = load(incidence, 3, 0, HALF, "inc")
         inc_rows[0, HALF] = load(incidence, 0, HALF, EDGES, "inc")
         load_w1()
@@ -161,6 +161,11 @@ def tile_heterogeneoustemporalhypergraphnn_pa_kernel(
 
         def release_gpsimd():
             nc.scalar.copy(out=attn_late[:], in_=attn[:])
+
+        def warm_tensor_clock():
+            scratch = psum.tile([P, CHANNELS], F32, name="scratch", tag="bank")
+            for i in range(3):
+                nc.tensor.matmul(scratch[:], lhsT=ones_bf16[:], rhs=bias_row[:], start=True, stop=True)
 
         feat_grouped = [
             keep.tile([P, PACK, P, PACK], BF16, name="feat_grouped%d" % c, align_bytes=64)
@@ -292,14 +297,15 @@ def tile_heterogeneoustemporalhypergraphnn_pa_kernel(
 
         features(0)
         softmax = softmax_partition_max()
-        features(1)
-        softmax = softmax_exp(*softmax)
+        warm_tensor_clock()
         incidence_piece(0, 0, HALF)
+        softmax = softmax_exp(*softmax)
+        features(1)
         softmax_normalise(softmax)
-        features(2)
         incidence_piece(1, 0, HALF)
-        features(3)
+        features(2)
         incidence_piece(2, 0, HALF)
+        features(3)
         incidence_piece(3, 0, HALF)
         incidence_piece(0, HALF, EDGES)
         release_gpsimd()

from contextlib import ExitStack

import concourse.mybir as mybir
from concourse.masks import make_identity

BF16 = mybir.dt.bfloat16
F32 = mybir.dt.float32
I32 = mybir.dt.int32
U32 = mybir.dt.uint32
U8 = mybir.dt.uint8
FP8X4 = mybir.dt.float8_e4m3fn_x4
ALU = mybir.AluOpType
ACT = mybir.ActivationFunctionType
AXIS = mybir.AxisListType

P = 128
PACK = 4
K_PASS = P * PACK
BANK = 512

NODES = 2048
EDGES = 1024
CHANNELS = 512
PASSES = NODES // K_PASS
TILES = EDGES // P
RUN = 4

HALF = 512

FEAT_SCALAR_Q = 64
INC_SCALAR_SHARE = 0.53125

FLOPS = 2 * NODES * EDGES * CHANNELS + 2 * EDGES * CHANNELS * CHANNELS


def tile_heterogeneoustemporalhypergraphnn_pa_kernel(
    tc, node_features, incidence, W1_words, W1_scales, b1, edge_attention, out
):
    nc = tc.nc
    with ExitStack() as ctx:
        keep = ctx.enter_context(tc.tile_pool(name="keep", bufs=1))
        psum = ctx.enter_context(tc.psum_pool(name="psum", bufs=8))
        ctx.enter_context(tc.manual_schedule())

        warm = keep.tile([P, 1], F32)
        nc.vector.memset(warm[:], 0.0)
        nc.scalar.activation(out=warm[:], in_=warm[:], func=ACT.Exp)

        def load(source, c, first, last, name):
            rows = keep.tile([P, PACK, last - first], BF16, name="%s_%d_%d" % (name, c, first))
            nc.sync.dma_start(
                out=rows[:],
                in_=source[c * K_PASS : (c + 1) * K_PASS, first:last].rearrange("(p j) w -> p j w", j=PACK),
            )
            return rows

        feat_rows = {}
        inc_rows = {}
        feat_rows[0, 0] = load(node_features, 0, 0, CHANNELS, "feat")

        logit_rows = keep.tile([P, P], BF16)
        nc.vector.memset(logit_rows[:], 0.0)
        nc.sync.dma_start(
            out=logit_rows[0:TILES, :], in_=edge_attention.rearrange("(s p) -> s p", p=P)
        )
        bias_row = keep.tile([P, CHANNELS], BF16)
        nc.vector.memset(bias_row[:], 0.0)
        nc.sync.dma_start(out=bias_row[0:1, :], in_=b1.rearrange("(o n) -> o n", o=1))

        w1_codes = keep.tile([P, CHANNELS], U32, align_bytes=64)
        w1_scales = keep.tile([P, CHANNELS], U8, align_bytes=64)
        nc.vector.memset(w1_scales[:].bitcast(I32), 0)

        def load_w1():
            nc.sync.dma_start(
                out=w1_codes[:].bitcast(I32),
                in_=W1_words[0].rearrange("p n t -> p (n t)").bitcast(I32),
            )
            for quadrant in range(4):
                nc.sync.dma_start(
                    out=w1_scales[32 * quadrant : 32 * quadrant + 4, :].bitcast(I32),
                    in_=W1_scales[0, 4 * quadrant : 4 * quadrant + 4, :].bitcast(I32),
                )

        inc_rows[0, 0] = load(incidence, 0, 0, HALF, "inc")
        feat_rows[1, 0] = load(node_features, 1, 0, CHANNELS, "feat")
        inc_rows[1, 0] = load(incidence, 1, 0, HALF, "inc")
        feat_rows[2, 0] = load(node_features, 2, 0, CHANNELS, "feat")
        inc_rows[2, 0] = load(incidence, 2, 0, HALF, "inc")
        feat_rows[3, 0] = load(node_features, 3, 0, CHANNELS, "feat")
        inc_rows[3, 0] = load(incidence, 3, 0, HALF, "inc")
        inc_rows[0, HALF] = load(incidence, 0, HALF, EDGES, "inc")
        load_w1()
        inc_rows[1, HALF] = load(incidence, 1, HALF, EDGES, "inc")
        inc_rows[2, HALF] = load(incidence, 2, HALF, EDGES, "inc")
        inc_rows[3, HALF] = load(incidence, 3, HALF, EDGES, "inc")

        ident_bf16 = keep.tile([P, P], BF16)
        make_identity(nc, ident_bf16[:])
        neg_ident = keep.tile([P, P], F32)
        make_identity(nc, neg_ident[:])
        nc.gpsimd.tensor_scalar(out=neg_ident[:], in0=neg_ident[:], scalar1=-1.0, scalar2=0.0, op0=ALU.mult, op1=ALU.add)
        ones_bf16 = keep.tile([P, P], BF16)
        nc.vector.memset(ones_bf16[:], 1.0)
        ones_f32 = keep.tile([P, P], F32)
        nc.vector.memset(ones_f32[:], 1.0)

        exp_cols = keep.tile([P, TILES], F32)
        attn = keep.tile([P, TILES], F32)
        bias_all = keep.tile([P, CHANNELS], F32)

        def softmax_partition_max():
            logit_cols = psum.tile([P, P], BF16, name="logit_cols", tag="bank")
            nc.tensor.transpose(logit_cols[:], logit_rows[:], ident_bf16[:])
            part_max = keep.tile([P, 1], F32)
            nc.vector.reduce_max(out=part_max[:], in_=logit_cols[:, 0:TILES], axis=AXIS.X)
            bias_ps = psum.tile([P, CHANNELS], F32, name="bias_ps", tag="bank")
            nc.tensor.matmul(bias_ps[:], lhsT=ones_bf16[:], rhs=bias_row[:], start=True, stop=True)
            neg_maxima = psum.tile([P, P], F32, name="neg_maxima", tag="bank")
            nc.tensor.matmul(
                neg_maxima[:], lhsT=part_max[:].to_broadcast([P, P]), rhs=neg_ident[:], start=True, stop=True
            )
            return logit_cols, bias_ps, neg_maxima

        def softmax_exp(logit_cols, bias_ps, neg_maxima):
            neg_max = keep.tile([P, 1], F32)
            nc.vector.tensor_reduce(out=neg_max[:], in_=neg_maxima[:], axis=AXIS.X, op=ALU.min)
            nc.scalar.copy(out=bias_all[:], in_=bias_ps[:])
            part_sum = keep.tile([P, 1], F32)
            nc.scalar.activation(
                out=exp_cols[:], in_=logit_cols[:, 0:TILES], func=ACT.Exp, bias=neg_max[:], scale=1.0,
                accum_out=part_sum[:],
            )
            total = psum.tile([P, P], F32, name="total", tag="bank")
            nc.tensor.matmul(total[:, 0:1], lhsT=ones_f32[:], rhs=part_sum[:], start=True, stop=True)
            return total

        def softmax_normalise(total):
            inv_sum = keep.tile([P, 1], F32)
            nc.vector.reciprocal(out=inv_sum[:], in_=total[:, 0:1])
            nc.vector.tensor_scalar_mul(out=attn[:], in0=exp_cols[:], scalar1=inv_sum[:])

        bias_attn = []

        def scale_bias():
            s = len(bias_attn)
            scaled = keep.tile([P, CHANNELS], F32, name="bias_attn%d" % s)
            nc.vector.tensor_scalar_mul(out=scaled[:], in0=bias_all[:], scalar1=attn[:, s : s + 1])
            bias_attn.append(scaled)

        attn_late = keep.tile([P, TILES], F32)

        def scale_bias_late():
            s = len(bias_attn)
            scaled = keep.tile([P, CHANNELS], F32, name="bias_attn%d" % s)
            nc.gpsimd.tensor_scalar(
                out=scaled[:], in0=bias_all[:], scalar1=attn_late[:, s : s + 1], scalar2=0.0,
                op0=ALU.mult, op1=ALU.add,
            )
            bias_attn.append(scaled)

        def release_gpsimd():
            nc.scalar.copy(out=attn_late[:], in_=attn[:])

        def warm_tensor_clock():
            scratch = psum.tile([P, CHANNELS], F32, name="scratch", tag="bank")
            for i in range(3):
                nc.tensor.matmul(scratch[:], lhsT=ones_bf16[:], rhs=bias_row[:], start=True, stop=True)

        feat_grouped = [
            keep.tile([P, PACK, P, PACK], BF16, name="feat_grouped%d" % c, align_bytes=64)
            for c in range(PASSES)
        ]
        feat_codes = [
            keep.tile([P, CHANNELS], U32, name="feat_codes%d" % c, align_bytes=64) for c in range(PASSES)
        ]
        feat_scales = [
            keep.tile([P, CHANNELS], U8, name="feat_scales%d" % c, align_bytes=64) for c in range(PASSES)
        ]

        def columns(rows, c, first, last):
            start = max(s for (k, s) in rows if k == c and s <= first)
            return rows[c, start][:, :, first - start : last - start]

        def regroup_features(c):
            for copy, first, last in (
                (nc.scalar.copy, 0, FEAT_SCALAR_Q),
                (nc.vector.tensor_copy, FEAT_SCALAR_Q, P),
            ):
                copy(
                    out=feat_grouped[c][:, :, first:last, :].rearrange("p t q j -> p q j t"),
                    in_=columns(feat_rows, c, PACK * first, PACK * last).rearrange(
                        "p j (q t) -> p q j t", t=PACK
                    ),
                )

        def quantise_features(c):
            nc.vector.quantize_mx(
                out=feat_codes[c][:].bitcast(FP8X4),
                scales=feat_scales[c][:],
                in_=feat_grouped[c][:].rearrange("p t q j -> p (t q j)"),
            )

        inc_grouped = [
            keep.tile([P, EDGES, PACK], BF16, name="inc_grouped%d" % c, align_bytes=64) for c in range(PASSES)
        ]
        inc_codes = [keep.tile([P, EDGES], U32, name="inc_codes%d" % c, align_bytes=64) for c in range(PASSES)]
        inc_scales = [keep.tile([P, EDGES], U8, name="inc_scales%d" % c, align_bytes=64) for c in range(PASSES)]

        def regroup_incidence(c, start, end):
            cut = start + int((end - start) * INC_SCALAR_SHARE) // 16 * 16
            for copy, first, last in ((nc.scalar.copy, start, cut), (nc.vector.tensor_copy, cut, end)):
                copy(
                    out=inc_grouped[c][:, first:last, :].rearrange("p (g i) j -> p g j i", i=RUN),
                    in_=columns(inc_rows, c, first, last).rearrange("p j (g i) -> p g j i", i=RUN),
                )

        agg_ps = []

        def quantise_incidence_and_multiply(c, start, end):
            nc.vector.quantize_mx(
                out=inc_codes[c][:, start:end].bitcast(FP8X4),
                scales=inc_scales[c][:, start:end],
                in_=inc_grouped[c][:, start:end, :].rearrange("p e j -> p (e j)"),
            )
            for s in range(start // P, end // P):
                if c == 0:
                    agg_ps.append(psum.tile([P, PACK, P], F32, name="agg_ps%d" % s, tag="bank"))
                for t in range(PACK):
                    nc.tensor.matmul_mx(
                        out=agg_ps[s][:, t, :],
                        lhsT=feat_codes[c][:, t * P : (t + 1) * P].bitcast(FP8X4),
                        lhsT_scale=feat_scales[c][:, t * P : (t + 1) * P],
                        rhs=inc_codes[c][:, s * P : (s + 1) * P].bitcast(FP8X4),
                        rhs_scale=inc_scales[c][:, s * P : (s + 1) * P],
                        start=(c == 0 and t == 0),
                        stop=(c == PASSES - 1 and t == PACK - 1),
                    )

        agg_grouped = [
            keep.tile([P, P, PACK], BF16, name="agg_grouped%d" % s, align_bytes=64) for s in range(TILES)
        ]
        lin_ps = []

        def agg_out(s, copy):
            copy(out=agg_grouped[s][:], in_=agg_ps[s][:].rearrange("p t e -> p e t"))

        def quantise_agg_and_multiply(s):
            agg_codes = keep.tile([P, P], U32, name="agg_codes%d" % s, align_bytes=64)
            agg_scales = keep.tile([P, P], U8, name="agg_scales%d" % s, align_bytes=64)
            nc.vector.quantize_mx(
                out=agg_codes[:].bitcast(FP8X4),
                scales=agg_scales[:],
                in_=agg_grouped[s][:].rearrange("p e t -> p (e t)"),
            )
            lin = psum.tile([P, CHANNELS], F32, name="lin%d" % s, tag="bank")
            nc.tensor.matmul_mx(
                out=lin[:],
                lhsT=agg_codes[:].bitcast(FP8X4),
                lhsT_scale=agg_scales[:],
                rhs=w1_codes[:].bitcast(FP8X4),
                rhs_scale=w1_scales[:],
                start=True,
                stop=True,
            )
            lin_ps.append(lin)

        def finish(s):
            result = keep.tile([P, CHANNELS], F32, name="result%d" % s)
            nc.vector.scalar_tensor_tensor(
                out=result[:], in0=lin_ps[s][:], scalar=attn[:, s : s + 1], in1=bias_attn[s][:],
                op0=ALU.mult, op1=ALU.add,
            )
            nc.sync.dma_start(out=out[s * P : (s + 1) * P, :], in_=result[:])

        waiting = []

        def step(regroup, quantise, *piece):
            regroup(*piece)
            if waiting:
                waiting.pop(0)()
            waiting.append(lambda: quantise(*piece))

        def features(c):
            step(regroup_features, quantise_features, c)

        def incidence_piece(c, start, end):
            step(regroup_incidence, quantise_incidence_and_multiply, c, start, end)

        def way_out(s):
            if s < TILES:
                agg_out(s, nc.scalar.copy)
            if 1 <= s <= TILES:
                quantise_agg_and_multiply(s - 1)
            if 2 <= s:
                finish(s - 2)

        features(0)
        softmax = softmax_partition_max()
        warm_tensor_clock()
        incidence_piece(0, 0, HALF)
        softmax = softmax_exp(*softmax)
        features(1)
        softmax_normalise(softmax)
        incidence_piece(1, 0, HALF)
        features(2)
        incidence_piece(2, 0, HALF)
        features(3)
        incidence_piece(3, 0, HALF)
        incidence_piece(0, HALF, EDGES)
        release_gpsimd()
        scale_bias_late()
        scale_bias_late()
        scale_bias_late()
        scale_bias_late()
        scale_bias_late()
        scale_bias_late()
        scale_bias_late()
        scale_bias_late()
        agg_out(0, nc.scalar.copy)
        incidence_piece(1, HALF, EDGES)
        agg_out(1, nc.scalar.copy)
        quantise_agg_and_multiply(0)
        incidence_piece(2, HALF, EDGES)
        agg_out(2, nc.scalar.copy)
        quantise_agg_and_multiply(1)
        finish(0)
        incidence_piece(3, 512, 768)
        agg_out(3, nc.scalar.copy)
        quantise_agg_and_multiply(2)
        finish(1)
        incidence_piece(3, 768, 1024)
        quantise_agg_and_multiply(3)
        waiting.pop(0)()
        agg_out(4, nc.scalar.copy)
        finish(2)
        agg_out(5, nc.scalar.copy)
        quantise_agg_and_multiply(4)
        finish(3)
        agg_out(6, nc.scalar.copy)
        quantise_agg_and_multiply(5)
        finish(4)
        agg_out(7, nc.scalar.copy)
        quantise_agg_and_multiply(6)
        finish(5)
        quantise_agg_and_multiply(7)
        finish(6)
        finish(7)
